import numpy as np
import ml_dtypes


def mxq(x, axis, fmt="e4m3"):
    dtype, down = {"e4m3": (ml_dtypes.float8_e4m3fn, 7), "e5m2": (ml_dtypes.float8_e5m2, 14)}[fmt]
    v = np.moveaxis(np.asarray(x, np.float32).astype(ml_dtypes.bfloat16).astype(np.float64), axis, -1)
    blocks = v.reshape(v.shape[:-1] + (-1, 32))
    amax = np.abs(blocks).max(-1, keepdims=True)
    byte = np.maximum(np.where(amax > 0, np.frexp(amax)[1] - 1 + 127, 0) - down, 1)
    scale = np.exp2(byte - 127.0)
    codes = (blocks / scale).astype(np.float32).astype(dtype).astype(np.float64)
    return np.moveaxis((codes * scale).reshape(v.shape), -1, axis)


WIDE = False


def mx_kscale(k):
    if not WIDE:
        return np.ones(k)
    levels = np.array([10, -10, 5, -5, 0])
    a = np.random.permutation(np.resize(levels, k // 512 * 4)).reshape(k // 512, 4)
    idx = np.arange(k)
    return np.exp2(a[idx // 512, idx % 128 // 32])


BF16 = ml_dtypes.bfloat16


def bf(x):
    return np.asarray(x, np.float32).astype(BF16)


def f64(x):
    return np.asarray(x).astype(np.float64)


B, N, D, F, M1, M2 = 4, 512, 512, 512, 3, 5
EPS = 1e-12


def erf(z):
    a = np.clip(z, -6.0, 6.0)
    a2 = 2.0 * a * a
    term = a.copy()
    tot = a.copy()
    for k in range(1, 120):
        term = term * (a2 / (2 * k + 1))
        tot = tot + term
    return 2.0 / np.sqrt(np.pi) * np.exp(-a * a) * tot


def gelu(v):
    return 0.5 * v * (1.0 + erf(v / np.sqrt(2.0)))


def setup_inputs():
    s = mx_kscale(D)
    return {'x': bf(np.random.standard_normal((B, N, D, M2)) * s[:, None]),
            'w_in': bf(np.random.standard_normal((D, F)) / np.sqrt(D) / s[:, None]),
            'scale': bf(1.0 + 0.1 * np.random.standard_normal((1, 1, F))),
            'bias': bf(0.3 * np.random.standard_normal((1, 1, F))),
            'w_out': bf(np.random.standard_normal((F, D)) / np.sqrt(F))}


def reference(x, w_in, scale, bias, w_out):
    xq = mxq(f64(x), 2, 'e4m3')
    h = np.swapaxes(np.swapaxes(xq, -1, -2) @ mxq(f64(w_in), 0, 'e4m3'), -1, -2)
    norm = np.maximum(np.sqrt(np.sum(h * h, axis=-1, keepdims=True)), EPS)
    phase = h / norm
    gated = gelu(norm[..., 0] * f64(scale) + f64(bias))[..., None]
    g = gated * phase
    y = np.swapaxes(mxq(g, 2, 'e4m3'), -1, -2) @ mxq(f64(w_out), 0, 'e4m3')
    return np.swapaxes(y, -1, -2)

@@ -1,0 +1,284 @@
+from contextlib import ExitStack
+
+import concourse.mybir as mybir
+from concourse.masks import make_identity
+
+F32 = mybir.dt.float32
+BF16 = mybir.dt.bfloat16
+U32 = mybir.dt.uint32
+U8 = mybir.dt.uint8
+FP8X4 = mybir.dt.float8_e4m3fn_x4
+ACT = mybir.ActivationFunctionType
+ALU = mybir.AluOpType
+
+P = 128
+PACK = 4
+TOKENS = 4 * 512
+D = 512
+F = 512
+M2 = 5
+ROW = D * M2
+EPS = 1e-12
+
+TILES = TOKENS // P
+PAIR = 2 * P
+PAIRS = TOKENS // PAIR
+CHUNK = 4 * P
+CHUNKS = TOKENS // CHUNK
+D_STEP = 64
+
+FLOPS = 2 * 2 * TOKENS * M2 * D * F
+
+
+def tile_feedforwardse3_pb_t_kernel(tc, x, w_in, scale, bias, w_out, out):
+    nc = tc.nc
+    x_rows = x.rearrange("b n d m -> (b n) (d m)")
+    out_rows = out.rearrange("b n d m -> (b n) (d m)")
+
+    with ExitStack() as ctx:
+        ctx.enter_context(tc.manual_schedule())
+        keep = ctx.enter_context(tc.tile_pool(name="keep", bufs=1))
+
+        ident = keep.tile([P, P], F32)
+        make_identity(nc, ident[:])
+
+        w_in_codes = keep.tile([P, F], U32, align_bytes=64)
+        w_in_scales = keep.tile([P, F], U8, align_bytes=64)
+        w_out_codes = keep.tile([P, D], U32, align_bytes=64)
+        w_out_scales = keep.tile([P, D], U8, align_bytes=64)
+        x_codes = keep.tile([P, M2, TOKENS], U32, align_bytes=64)
+        x_scales = keep.tile([P, M2, TOKENS], U8, align_bytes=64)
+
+        norm = keep.tile([P, PACK, TOKENS], F32)
+        factor = keep.tile([P, PACK, TOKENS], F32)
+        scale_f32 = keep.tile([P, PACK], F32)
+        bias_f32 = keep.tile([P, PACK], F32)
+
+        with tc.tile_pool(name="weights", bufs=1) as weights, tc.tile_pool(
+            name="loaded", bufs=3
+        ) as loaded_pool, tc.tile_pool(name="split", bufs=2) as split_pool, tc.tile_pool(
+            name="grouped", bufs=4
+        ) as grouped_pool, tc.tile_pool(name="squares", bufs=2) as square_pool, tc.psum_pool(
+            name="xt", bufs=3
+        ) as xt_pool, tc.psum_pool(name="ht", bufs=3) as ht_pool, tc.psum_pool(
+            name="sums", bufs=2
+        ) as sum_pool:
+
+            def load_pair(q):
+                x_sb = loaded_pool.tile([P, 2, ROW], BF16)
+                nc.sync.dma_start(
+                    out=x_sb[:],
+                    in_=x_rows[q * PAIR : (q + 1) * PAIR, :].rearrange("(a p) c -> p a c", p=P),
+                )
+                return x_sb
+
+            def split_components(x_sb):
+                x_split = split_pool.tile([P, 2, 2, M2, 2 * P], BF16)
+                for a in range(2):
+                    nc.vector.tensor_copy(
+                        out=x_split[:, a].rearrange("p u m (q e) -> p u m q e", e=2),
+                        in_=x_sb[:, a, :].rearrange("p (q u e m) -> p u m q e", u=2, e=2, m=M2),
+                    )
+                return x_split
+
+            def quantise_x(q, m, grouped):
+                cols = slice(q * PAIR, (q + 1) * PAIR)
+                nc.vector.quantize_mx(
+                    out=x_codes[:, m, cols].bitcast(FP8X4),
+                    scales=x_scales[:, m, cols],
+                    in_=grouped[:].rearrange("p t i -> p (t i)"),
+                )
+
+            def pack_pair(q, x_split):
+                words = x_split[:].bitcast(F32)
+                groups = []
+                for m in range(M2):
+                    xt = xt_pool.tile([P, 2, 2, P], F32)
+                    for a in range(2):
+                        for u in range(2):
+                            nc.tensor.transpose(xt[:, a, u, :], words[:, a, u, m, :], ident[:])
+                    grouped = grouped_pool.tile([P, PAIR, PACK], BF16, align_bytes=64)
+                    copy = nc.scalar.copy if m % 2 == 0 else nc.vector.tensor_copy
+                    copy(
+                        out=grouped[:].bitcast(F32).rearrange("p (a t) u -> p a t u", a=2),
+                        in_=xt[:].rearrange("p a u t -> p a t u"),
+                    )
+                    groups.append(grouped)
+                    if m > 0:
+                        quantise_x(q, m - 1, groups[m - 1])
+                quantise_x(q, M2 - 1, groups[M2 - 1])
+
+            def square_h(i):
+                cols = slice(i * P, (i + 1) * P)
+                squares = []
+                for m in range(M2):
+                    ht = ht_pool.tile([P, F], F32)
+                    nc.tensor.matmul_mx(
+                        out=ht[:],
+                        lhsT=x_codes[:, m, cols].bitcast(FP8X4),
+                        lhsT_scale=x_scales[:, m, cols],
+                        rhs=w_in_codes[:].bitcast(FP8X4),
+                        rhs_scale=w_in_scales[:],
+                        start=True,
+                        stop=True,
+                    )
+                    sq = square_pool.tile([P, F], F32, name="sq%d" % m)
+                    nc.scalar.activation(out=sq[:], in_=ht[:], func=ACT.Square)
+                    squares.append(sq)
+                return squares
+
+            def sum_squares(i, squares):
+                cols = slice(i * P, (i + 1) * P)
+                sums = sum_pool.tile([P, PACK, P], F32)
+                for j in range(PACK):
+                    for m in range(M2):
+                        nc.tensor.matmul(
+                            out=sums[:, j, :],
+                            lhsT=squares[m][:, j * P : (j + 1) * P],
+                            rhs=ident[:],
+                            is_transpose=True,
+                            start=(m == 0),
+                            stop=(m == M2 - 1),
+                        )
+                nc.vector.tensor_scalar_max(out=norm[:, :, cols], in0=sums[:], scalar1=EPS * EPS)
+
+            def take_root(q):
+                cols = slice(q * PAIR, (q + 1) * PAIR)
+                nc.scalar.activation(
+                    out=factor[:, :, cols], in_=norm[:, :, cols], func=ACT.Abs_reciprocal_sqrt
+                )
+                nc.vector.tensor_mul(
+                    out=norm[:, :, cols], in0=norm[:, :, cols], in1=factor[:, :, cols]
+                )
+
+            w_in_raw = weights.tile([P, PACK, F], BF16)
+            nc.sync.dma_start(out=w_in_raw[:], in_=w_in.rearrange("(p i) f -> p i f", i=PACK))
+            w_out_raw = weights.tile([P, PACK, D], BF16)
+            nc.sync.dma_start(out=w_out_raw[:], in_=w_out.rearrange("(p j) d -> p j d", j=PACK))
+            loaded = {0: load_pair(0), 1: load_pair(1)}
+            scale_raw = weights.tile([P, PACK], BF16)
+            nc.sync.dma_start(out=scale_raw[:], in_=scale.rearrange("a b (p j) -> (a b p) j", j=PACK))
+            bias_raw = weights.tile([P, PACK], BF16)
+            nc.sync.dma_start(out=bias_raw[:], in_=bias.rearrange("a b (p j) -> (a b p) j", j=PACK))
+            nc.gpsimd.tensor_copy(out=scale_f32[:], in_=scale_raw[:])
+            nc.gpsimd.tensor_copy(out=bias_f32[:], in_=bias_raw[:])
+
+            w_in_grouped = weights.tile([P, PACK, P, PACK], BF16, align_bytes=64)
+            nc.vector.tensor_copy(
+                out=w_in_grouped[:], in_=w_in_raw[:].rearrange("p i (q j) -> p j q i", j=PACK)
+            )
+            w_out_grouped = weights.tile([P, D, PACK], BF16, align_bytes=64)
+            nc.vector.tensor_copy(out=w_out_grouped[:], in_=w_out_raw[:].rearrange("p j d -> p d j"))
+            nc.vector.quantize_mx(
+                out=w_in_codes[:].bitcast(FP8X4),
+                scales=w_in_scales[:],
+                in_=w_in_grouped[:].rearrange("p j q i -> p (j q i)"),
+            )
+            nc.vector.quantize_mx(
+                out=w_out_codes[:].bitcast(FP8X4),
+                scales=w_out_scales[:],
+                in_=w_out_grouped[:].rearrange("p d j -> p (d j)"),
+            )
+            split = {0: split_components(loaded[0])}
+
+            squares = {}
+            for s in range(PAIRS + 2):
+                if s + 2 < PAIRS:
+                    loaded[s + 2] = load_pair(s + 2)
+                if s < PAIRS:
+                    pack_pair(s, split[s])
+                if s + 1 < PAIRS:
+                    split[s + 1] = split_components(loaded[s + 1])
+                for i in (2 * (s - 1), 2 * (s - 1) + 1):
+                    if 0 <= i < TILES:
+                        squares[i] = square_h(i)
+                    if 0 <= i - 1 < TILES:
+                        sum_squares(i - 1, squares[i - 1])
+                if s >= 2:
+                    take_root(s - 2)
+
+        with tc.tile_pool(name="g", bufs=2) as g_pool, tc.tile_pool(
+            name="result", bufs=3
+        ) as result_pool, tc.psum_pool(name="h", bufs=4) as h_pool, tc.psum_pool(
+            name="y", bufs=4
+        ) as y_pool:
+
+            def gate(c):
+                cols = slice(c * CHUNK, (c + 1) * CHUNK)
+                for j in range(PACK):
+                    nc.scalar.activation(
+                        out=norm[:, j, cols],
+                        in_=norm[:, j, cols],
+                        func=ACT.Gelu,
+                        scale=scale_f32[:, j : j + 1],
+                        bias=bias_f32[:, j : j + 1],
+                    )
+                nc.vector.tensor_mul(
+                    out=factor[:, :, cols], in0=factor[:, :, cols], in1=norm[:, :, cols]
+                )
+
+            def quantise_g(m, g_grouped, g_codes, g_scales):
+                nc.vector.quantize_mx(
+                    out=g_codes[:, m, :].bitcast(FP8X4),
+                    scales=g_scales[:, m, :],
+                    in_=g_grouped[:, m].rearrange("p t j -> p (t j)"),
+                )
+
+            def hidden(i):
+                cols = slice(i * P, (i + 1) * P)
+                g_grouped = g_pool.tile([P, M2, P, PACK], BF16, align_bytes=64)
+                g_codes = g_pool.tile([P, M2, P], U32, align_bytes=64)
+                g_scales = g_pool.tile([P, M2, P], U8, align_bytes=64)
+                for m in range(M2):
+                    h = h_pool.tile([P, PACK, P], F32)
+                    for j in range(PACK):
+                        nc.tensor.matmul_mx(
+                            out=h[:, j, :],
+                            lhsT=w_in_codes[:, j * P : (j + 1) * P].bitcast(FP8X4),
+                            lhsT_scale=w_in_scales[:, j * P : (j + 1) * P],
+                            rhs=x_codes[:, m, cols].bitcast(FP8X4),
+                            rhs_scale=x_scales[:, m, cols],
+                            start=True,
+                            stop=True,
+                        )
+                    nc.vector.tensor_tensor(
+                        out=g_grouped[:, m],
+                        in0=h[:].rearrange("p j t -> p t j"),
+                        in1=factor[:, :, cols].rearrange("p j t -> p t j"),
+                        op=ALU.mult,
+                    )
+                    if m > 0:
+                        quantise_g(m - 1, g_grouped, g_codes, g_scales)
+                quantise_g(M2 - 1, g_grouped, g_codes, g_scales)
+                return g_codes, g_scales
+
+            def project(i, g_codes, g_scales):
+                result = result_pool.tile([P, D // D_STEP, D_STEP, M2], F32)
+                for k in range(D // D_STEP):
+                    d_cols = slice(k * D_STEP, (k + 1) * D_STEP)
+                    y = y_pool.tile([P, M2, D_STEP], F32)
+                    for m in range(M2):
+                        nc.tensor.matmul_mx(
+                            out=y[:, m, :],
+                            lhsT=g_codes[:, m, :].bitcast(FP8X4),
+                            lhsT_scale=g_scales[:, m, :],
+                            rhs=w_out_codes[:, d_cols].bitcast(FP8X4),
+                            rhs_scale=w_out_scales[:, d_cols],
+                            start=True,
+                            stop=True,
+                        )
+                    nc.scalar.copy(out=result[:, k], in_=y[:].rearrange("p m d -> p d m"))
+                nc.sync.dma_start(
+                    out=out_rows[i * P : (i + 1) * P, :],
+                    in_=result[:].rearrange("p k d m -> p (k d m)"),
+                )
+
+            gate(0)
+            g_of = {}
+            for i in range(TILES + 1):
+                if i < TILES:
+                    g_of[i] = hidden(i)
+                    if i % (CHUNK // P) == 0 and i // (CHUNK // P) + 1 < CHUNKS:
+                        gate(i // (CHUNK // P) + 1)
+                if i >= 1:
+                    project(i - 1, g_of[i - 1][0], g_of[i - 1][1])

@@ -25,7 +25,6 @@ PAIR = 2 * P
 PAIRS = TOKENS // PAIR
 CHUNK = 4 * P
 CHUNKS = TOKENS // CHUNK
-D_STEP = 64
 
 FLOPS = 2 * 2 * TOKENS * M2 * D * F
 
@@ -36,7 +35,6 @@ def tile_feedforwardse3_pb_t_kernel(tc, x, w_in, scale, bias, w_out, out):
     out_rows = out.rearrange("b n d m -> (b n) (d m)")
 
     with ExitStack() as ctx:
-        ctx.enter_context(tc.manual_schedule())
         keep = ctx.enter_context(tc.tile_pool(name="keep", bufs=1))
 
         ident = keep.tile([P, P], F32)
@@ -198,10 +196,10 @@ def tile_feedforwardse3_pb_t_kernel(tc, x, w_in, scale, bias, w_out, out):
                     take_root(s - 2)
 
         with tc.tile_pool(name="g", bufs=2) as g_pool, tc.tile_pool(
-            name="result", bufs=3
-        ) as result_pool, tc.psum_pool(name="h", bufs=4) as h_pool, tc.psum_pool(
-            name="y", bufs=4
-        ) as y_pool:
+            name="planes", bufs=2
+        ) as plane_pool, tc.tile_pool(name="result", bufs=3) as result_pool, tc.psum_pool(
+            name="h", bufs=4
+        ) as h_pool, tc.psum_pool(name="y", bufs=4) as y_pool:
 
             def gate(c):
                 cols = slice(c * CHUNK, (c + 1) * CHUNK)
@@ -253,24 +251,30 @@ def tile_feedforwardse3_pb_t_kernel(tc, x, w_in, scale, bias, w_out, out):
                 return g_codes, g_scales
 
             def project(i, g_codes, g_scales):
-                result = result_pool.tile([P, D // D_STEP, D_STEP, M2], F32)
-                for k in range(D // D_STEP):
-                    d_cols = slice(k * D_STEP, (k + 1) * D_STEP)
-                    y = y_pool.tile([P, M2, D_STEP], F32)
-                    for m in range(M2):
-                        nc.tensor.matmul_mx(
-                            out=y[:, m, :],
-                            lhsT=g_codes[:, m, :].bitcast(FP8X4),
-                            lhsT_scale=g_scales[:, m, :],
-                            rhs=w_out_codes[:, d_cols].bitcast(FP8X4),
-                            rhs_scale=w_out_scales[:, d_cols],
-                            start=True,
-                            stop=True,
-                        )
-                    nc.scalar.copy(out=result[:, k], in_=y[:].rearrange("p m d -> p d m"))
+                planes = plane_pool.tile([P, M2, D], F32)
+                for m in range(M2):
+                    y = y_pool.tile([P, D], F32)
+                    nc.tensor.matmul_mx(
+                        out=y[:],
+                        lhsT=g_codes[:, m, :].bitcast(FP8X4),
+                        lhsT_scale=g_scales[:, m, :],
+                        rhs=w_out_codes[:].bitcast(FP8X4),
+                        rhs_scale=w_out_scales[:],
+                        start=True,
+                        stop=True,
+                    )
+                    nc.scalar.copy(out=planes[:, m, :], in_=y[:])
+                result = result_pool.tile([P, D, M2], F32)
+                nc.gpsimd.tensor_scalar(
+                    out=result[:],
+                    in0=planes[:].rearrange("p m d -> p d m"),
+                    scalar1=1.0,
+                    scalar2=0.0,
+                    op0=ALU.mult,
+                    op1=ALU.add,
+                )
                 nc.sync.dma_start(
-                    out=out_rows[i * P : (i + 1) * P, :],
-                    in_=result[:].rearrange("p k d m -> p (k d m)"),
+                    out=out_rows[i * P : (i + 1) * P, :], in_=result[:].rearrange("p d m -> p (d m)")
                 )
 
             gate(0)

@@ -23,8 +23,9 @@ EPS = 1e-12
 TILES = TOKENS // P
 PAIR = 2 * P
 PAIRS = TOKENS // PAIR
-CHUNK = 4 * P
-CHUNKS = TOKENS // CHUNK
+WINDOW = 128
+KEEP = 96
+BLOCKS = -(-D // KEEP)
 
 FLOPS = 2 * 2 * TOKENS * M2 * D * F
 
@@ -35,22 +36,23 @@ def tile_feedforwardse3_pb_t_kernel(tc, x, w_in, scale, bias, w_out, out):
     out_rows = out.rearrange("b n d m -> (b n) (d m)")
 
     with ExitStack() as ctx:
-        keep = ctx.enter_context(tc.tile_pool(name="keep", bufs=1))
+        ctx.enter_context(tc.manual_schedule())
+        resident = ctx.enter_context(tc.tile_pool(name="resident", bufs=1))
 
-        ident = keep.tile([P, P], F32)
+        ident = resident.tile([P, P], F32)
         make_identity(nc, ident[:])
 
-        w_in_codes = keep.tile([P, F], U32, align_bytes=64)
-        w_in_scales = keep.tile([P, F], U8, align_bytes=64)
-        w_out_codes = keep.tile([P, D], U32, align_bytes=64)
-        w_out_scales = keep.tile([P, D], U8, align_bytes=64)
-        x_codes = keep.tile([P, M2, TOKENS], U32, align_bytes=64)
-        x_scales = keep.tile([P, M2, TOKENS], U8, align_bytes=64)
+        w_in_codes = resident.tile([P, F], U32, align_bytes=64)
+        w_in_scales = resident.tile([P, F], U8, align_bytes=64)
+        w_out_codes = resident.tile([P, BLOCKS, WINDOW], U32, align_bytes=64)
+        w_out_scales = resident.tile([P, BLOCKS, WINDOW], U8, align_bytes=64)
+        x_codes = resident.tile([P, M2, TOKENS], U32, align_bytes=64)
+        x_scales = resident.tile([P, M2, TOKENS], U8, align_bytes=64)
 
-        norm = keep.tile([P, PACK, TOKENS], F32)
-        factor = keep.tile([P, PACK, TOKENS], F32)
-        scale_f32 = keep.tile([P, PACK], F32)
-        bias_f32 = keep.tile([P, PACK], F32)
+        norm = resident.tile([P, PACK, TOKENS], F32)
+        factor = resident.tile([P, PACK, TOKENS], F32)
+        scale_f32 = resident.tile([P, PACK], F32)
+        bias_f32 = resident.tile([P, PACK], F32)
 
         with tc.tile_pool(name="weights", bufs=1) as weights, tc.tile_pool(
             name="loaded", bufs=3
@@ -58,8 +60,8 @@ def tile_feedforwardse3_pb_t_kernel(tc, x, w_in, scale, bias, w_out, out):
             name="grouped", bufs=4
         ) as grouped_pool, tc.tile_pool(name="squares", bufs=2) as square_pool, tc.psum_pool(
             name="xt", bufs=3
-        ) as xt_pool, tc.psum_pool(name="ht", bufs=3) as ht_pool, tc.psum_pool(
-            name="sums", bufs=2
+        ) as xt_pool, tc.psum_pool(name="ht", bufs=4) as ht_pool, tc.psum_pool(
+            name="sums", bufs=1
         ) as sum_pool:
 
             def load_pair(q):
@@ -165,18 +167,25 @@ def tile_feedforwardse3_pb_t_kernel(tc, x, w_in, scale, bias, w_out, out):
             nc.vector.tensor_copy(
                 out=w_in_grouped[:], in_=w_in_raw[:].rearrange("p i (q j) -> p j q i", j=PACK)
             )
-            w_out_grouped = weights.tile([P, D, PACK], BF16, align_bytes=64)
-            nc.vector.tensor_copy(out=w_out_grouped[:], in_=w_out_raw[:].rearrange("p j d -> p d j"))
+            w_out_grouped = weights.tile([P, BLOCKS, WINDOW, PACK], BF16, align_bytes=64)
+            nc.vector.memset(w_out_grouped[:, BLOCKS - 1], 0.0)
+            for b in range(BLOCKS):
+                width = min(WINDOW, D - b * KEEP)
+                nc.vector.tensor_copy(
+                    out=w_out_grouped[:, b, 0:width, :],
+                    in_=w_out_raw[:, :, b * KEEP : b * KEEP + width].rearrange("p j d -> p d j"),
+                )
             nc.vector.quantize_mx(
                 out=w_in_codes[:].bitcast(FP8X4),
                 scales=w_in_scales[:],
                 in_=w_in_grouped[:].rearrange("p j q i -> p (j q i)"),
             )
-            nc.vector.quantize_mx(
-                out=w_out_codes[:].bitcast(FP8X4),
-                scales=w_out_scales[:],
-                in_=w_out_grouped[:].rearrange("p d j -> p (d j)"),
-            )
+            for b in range(BLOCKS):
+                nc.vector.quantize_mx(
+                    out=w_out_codes[:, b, :].bitcast(FP8X4),
+                    scales=w_out_scales[:, b, :],
+                    in_=w_out_grouped[:, b].rearrange("p d j -> p (d j)"),
+                )
             split = {0: split_components(loaded[0])}
 
             squares = {}
@@ -196,13 +205,13 @@ def tile_feedforwardse3_pb_t_kernel(tc, x, w_in, scale, bias, w_out, out):
                     take_root(s - 2)
 
         with tc.tile_pool(name="g", bufs=2) as g_pool, tc.tile_pool(
-            name="planes", bufs=2
-        ) as plane_pool, tc.tile_pool(name="result", bufs=3) as result_pool, tc.psum_pool(
-            name="h", bufs=4
-        ) as h_pool, tc.psum_pool(name="y", bufs=4) as y_pool:
+            name="result", bufs=3
+        ) as result_pool, tc.psum_pool(name="h", bufs=4) as h_pool, tc.psum_pool(
+            name="y", bufs=4
+        ) as y_pool:
 
-            def gate(c):
-                cols = slice(c * CHUNK, (c + 1) * CHUNK)
+            def gate(q):
+                cols = slice(q * PAIR, (q + 1) * PAIR)
                 for j in range(PACK):
                     nc.scalar.activation(
                         out=norm[:, j, cols],
@@ -251,28 +260,24 @@ def tile_feedforwardse3_pb_t_kernel(tc, x, w_in, scale, bias, w_out, out):
                 return g_codes, g_scales
 
             def project(i, g_codes, g_scales):
-                planes = plane_pool.tile([P, M2, D], F32)
-                for m in range(M2):
-                    y = y_pool.tile([P, D], F32)
-                    nc.tensor.matmul_mx(
-                        out=y[:],
-                        lhsT=g_codes[:, m, :].bitcast(FP8X4),
-                        lhsT_scale=g_scales[:, m, :],
-                        rhs=w_out_codes[:].bitcast(FP8X4),
-                        rhs_scale=w_out_scales[:],
-                        start=True,
-                        stop=True,
-                    )
-                    nc.scalar.copy(out=planes[:, m, :], in_=y[:])
                 result = result_pool.tile([P, D, M2], F32)
-                nc.gpsimd.tensor_scalar(
-                    out=result[:],
-                    in0=planes[:].rearrange("p m d -> p d m"),
-                    scalar1=1.0,
-                    scalar2=0.0,
-                    op0=ALU.mult,
-                    op1=ALU.add,
-                )
+                for b in range(BLOCKS):
+                    kept = min(KEEP, D - b * KEEP)
+                    y = y_pool.tile([P, (M2 - 1) * KEEP + WINDOW], F32)
+                    for m in range(M2):
+                        nc.tensor.matmul_mx(
+                            out=y[:, m * KEEP : m * KEEP + WINDOW],
+                            lhsT=g_codes[:, m, :].bitcast(FP8X4),
+                            lhsT_scale=g_scales[:, m, :],
+                            rhs=w_out_codes[:, b, :].bitcast(FP8X4),
+                            rhs_scale=w_out_scales[:, b, :],
+                            start=True,
+                            stop=True,
+                        )
+                    nc.scalar.copy(
+                        out=result[:, b * KEEP : b * KEEP + kept, :],
+                        in_=y[:, 0 : M2 * KEEP].rearrange("p (m d) -> p d m", m=M2)[:, 0:kept, :],
+                    )
                 nc.sync.dma_start(
                     out=out_rows[i * P : (i + 1) * P, :], in_=result[:].rearrange("p d m -> p (d m)")
                 )
@@ -282,7 +287,7 @@ def tile_feedforwardse3_pb_t_kernel(tc, x, w_in, scale, bias, w_out, out):
             for i in range(TILES + 1):
                 if i < TILES:
                     g_of[i] = hidden(i)
-                    if i % (CHUNK // P) == 0 and i // (CHUNK // P) + 1 < CHUNKS:
-                        gate(i // (CHUNK // P) + 1)
+                    if i % 2 == 0 and i // 2 + 1 < PAIRS:
+                        gate(i // 2 + 1)
                 if i >= 1:
                     project(i - 1, g_of[i - 1][0], g_of[i - 1][1])

@@ -36,7 +36,6 @@ def tile_feedforwardse3_pb_t_kernel(tc, x, w_in, scale, bias, w_out, out):
     out_rows = out.rearrange("b n d m -> (b n) (d m)")
 
     with ExitStack() as ctx:
-        ctx.enter_context(tc.manual_schedule())
         resident = ctx.enter_context(tc.tile_pool(name="resident", bufs=1))
 
         ident = resident.tile([P, P], F32)

@@ -49,7 +49,7 @@ def tile_feedforwardse3_pb_t_kernel(tc, x, w_in, scale, bias, w_out, out):
         x_scales = resident.tile([P, M2, TOKENS], U8, align_bytes=64)
 
         norm = resident.tile([P, PACK, TOKENS], F32)
-        factor = resident.tile([P, PACK, TOKENS], F32)
+        rnorm = resident.tile([P, PACK, TOKENS], F32)
         scale_f32 = resident.tile([P, PACK], F32)
         bias_f32 = resident.tile([P, PACK], F32)
 
@@ -144,10 +144,10 @@ def tile_feedforwardse3_pb_t_kernel(tc, x, w_in, scale, bias, w_out, out):
             def take_root(q):
                 cols = slice(q * PAIR, (q + 1) * PAIR)
                 nc.scalar.activation(
-                    out=factor[:, :, cols], in_=norm[:, :, cols], func=ACT.Abs_reciprocal_sqrt
+                    out=rnorm[:, :, cols], in_=norm[:, :, cols], func=ACT.Abs_reciprocal_sqrt
                 )
                 nc.vector.tensor_mul(
-                    out=norm[:, :, cols], in0=norm[:, :, cols], in1=factor[:, :, cols]
+                    out=norm[:, :, cols], in0=norm[:, :, cols], in1=rnorm[:, :, cols]
                 )
 
             w_in_raw = weights.tile([P, PACK, F], BF16)
@@ -203,25 +203,30 @@ def tile_feedforwardse3_pb_t_kernel(tc, x, w_in, scale, bias, w_out, out):
                 if s >= 2:
                     take_root(s - 2)
 
-        with tc.tile_pool(name="g", bufs=2) as g_pool, tc.tile_pool(
-            name="result", bufs=3
-        ) as result_pool, tc.psum_pool(name="h", bufs=4) as h_pool, tc.psum_pool(
+        with tc.tile_pool(name="gate", bufs=3) as gate_pool, tc.tile_pool(
+            name="g", bufs=2
+        ) as g_pool, tc.tile_pool(name="result", bufs=3) as result_pool, tc.psum_pool(name="h", bufs=4) as h_pool, tc.psum_pool(
             name="y", bufs=4
         ) as y_pool:
 
             def gate(q):
                 cols = slice(q * PAIR, (q + 1) * PAIR)
+                gelu = gate_pool.tile([P, PACK, PAIR], F32)
                 for j in range(PACK):
                     nc.scalar.activation(
-                        out=norm[:, j, cols],
+                        out=gelu[:, j, :],
                         in_=norm[:, j, cols],
                         func=ACT.Gelu,
                         scale=scale_f32[:, j : j + 1],
                         bias=bias_f32[:, j : j + 1],
                     )
+                factor = gate_pool.tile([P, PAIR, PACK], F32)
                 nc.vector.tensor_mul(
-                    out=factor[:, :, cols], in0=factor[:, :, cols], in1=norm[:, :, cols]
+                    out=factor[:],
+                    in0=gelu[:].rearrange("p j t -> p t j"),
+                    in1=rnorm[:, :, cols].rearrange("p j t -> p t j"),
                 )
+                return factor
 
             def quantise_g(m, g_grouped, g_codes, g_scales):
                 nc.vector.quantize_mx(
@@ -230,7 +235,7 @@ def tile_feedforwardse3_pb_t_kernel(tc, x, w_in, scale, bias, w_out, out):
                     in_=g_grouped[:, m].rearrange("p t j -> p (t j)"),
                 )
 
-            def hidden(i):
+            def hidden(i, factor):
                 cols = slice(i * P, (i + 1) * P)
                 g_grouped = g_pool.tile([P, M2, P, PACK], BF16, align_bytes=64)
                 g_codes = g_pool.tile([P, M2, P], U32, align_bytes=64)
@@ -250,7 +255,7 @@ def tile_feedforwardse3_pb_t_kernel(tc, x, w_in, scale, bias, w_out, out):
                     nc.vector.tensor_tensor(
                         out=g_grouped[:, m],
                         in0=h[:].rearrange("p j t -> p t j"),
-                        in1=factor[:, :, cols].rearrange("p j t -> p t j"),
+                        in1=factor[:, (i % 2) * P : (i % 2 + 1) * P, :],
                         op=ALU.mult,
                     )
                     if m > 0:
@@ -281,12 +286,12 @@ def tile_feedforwardse3_pb_t_kernel(tc, x, w_in, scale, bias, w_out, out):
                     out=out_rows[i * P : (i + 1) * P, :], in_=result[:].rearrange("p d m -> p (d m)")
                 )
 
-            gate(0)
+            factors = {0: gate(0)}
             g_of = {}
             for i in range(TILES + 1):
                 if i < TILES:
-                    g_of[i] = hidden(i)
+                    g_of[i] = hidden(i, factors[i // 2])
                     if i % 2 == 0 and i // 2 + 1 < PAIRS:
-                        gate(i // 2 + 1)
+                        factors[i // 2 + 1] = gate(i // 2 + 1)
                 if i >= 1:
                     project(i - 1, g_of[i - 1][0], g_of[i - 1][1])

@@ -23,6 +23,8 @@ EPS = 1e-12
 TILES = TOKENS // P
 PAIR = 2 * P
 PAIRS = TOKENS // PAIR
+CHUNK = 4 * P
+CHUNKS = TOKENS // CHUNK
 WINDOW = 128
 KEEP = 96
 BLOCKS = -(-D // KEEP)
@@ -72,12 +74,15 @@ def tile_feedforwardse3_pb_t_kernel(tc, x, w_in, scale, bias, w_out, out):
                 return x_sb
 
             def split_components(x_sb):
-                x_split = split_pool.tile([P, 2, 2, M2, 2 * P], BF16)
+                x_split = split_pool.tile([P, 2, M2, D], BF16)
                 for a in range(2):
-                    nc.vector.tensor_copy(
-                        out=x_split[:, a].rearrange("p u m (q e) -> p u m q e", e=2),
-                        in_=x_sb[:, a, :].rearrange("p (q u e m) -> p u m q e", u=2, e=2, m=M2),
-                    )
+                    for planes in (slice(0, 3), slice(3, M2)):
+                        nc.vector.tensor_copy(
+                            out=x_split[:, a, planes, :].rearrange("p m (c i) -> p c m i", i=PACK),
+                            in_=x_sb[:, a, :].rearrange("p (c i m) -> p c m i", i=PACK, m=M2)[
+                                :, :, planes, :
+                            ],
+                        )
                 return x_split
 
             def quantise_x(q, m, grouped):
@@ -89,13 +94,13 @@ def tile_feedforwardse3_pb_t_kernel(tc, x, w_in, scale, bias, w_out, out):
                 )
 
             def pack_pair(q, x_split):
-                words = x_split[:].bitcast(F32)
+                words = x_split[:].bitcast(F32).rearrange("p a m (u q) -> p a m u q", u=2)
                 groups = []
                 for m in range(M2):
                     xt = xt_pool.tile([P, 2, 2, P], F32)
                     for a in range(2):
                         for u in range(2):
-                            nc.tensor.transpose(xt[:, a, u, :], words[:, a, u, m, :], ident[:])
+                            nc.tensor.transpose(xt[:, a, u, :], words[:, a, m, u, :], ident[:])
                     grouped = grouped_pool.tile([P, PAIR, PACK], BF16, align_bytes=64)
                     copy = nc.scalar.copy if m % 2 == 0 else nc.vector.tensor_copy
                     copy(
@@ -150,17 +155,22 @@ def tile_feedforwardse3_pb_t_kernel(tc, x, w_in, scale, bias, w_out, out):
                     out=norm[:, :, cols], in0=norm[:, :, cols], in1=rnorm[:, :, cols]
                 )
 
+            loaded = {0: load_pair(0)}
             w_in_raw = weights.tile([P, PACK, F], BF16)
-            nc.sync.dma_start(out=w_in_raw[:], in_=w_in.rearrange("(p i) f -> p i f", i=PACK))
+            nc.sync.dma_start(
+                out=w_in_raw[:].rearrange("p (u e) f -> p u e f", u=2),
+                in_=w_in.rearrange("(u p e) f -> p u e f", u=2, e=2),
+            )
+            loaded[1] = load_pair(1)
             w_out_raw = weights.tile([P, PACK, D], BF16)
             nc.sync.dma_start(out=w_out_raw[:], in_=w_out.rearrange("(p j) d -> p j d", j=PACK))
-            loaded = {0: load_pair(0), 1: load_pair(1)}
             scale_raw = weights.tile([P, PACK], BF16)
             nc.sync.dma_start(out=scale_raw[:], in_=scale.rearrange("a b (p j) -> (a b p) j", j=PACK))
             bias_raw = weights.tile([P, PACK], BF16)
             nc.sync.dma_start(out=bias_raw[:], in_=bias.rearrange("a b (p j) -> (a b p) j", j=PACK))
             nc.gpsimd.tensor_copy(out=scale_f32[:], in_=scale_raw[:])
             nc.gpsimd.tensor_copy(out=bias_f32[:], in_=bias_raw[:])
+            split = {0: split_components(loaded[0])}
 
             w_in_grouped = weights.tile([P, PACK, P, PACK], BF16, align_bytes=64)
             nc.vector.tensor_copy(
@@ -185,8 +195,6 @@ def tile_feedforwardse3_pb_t_kernel(tc, x, w_in, scale, bias, w_out, out):
                     scales=w_out_scales[:, b, :],
                     in_=w_out_grouped[:, b].rearrange("p d j -> p (d j)"),
                 )
-            split = {0: split_components(loaded[0])}
-
             squares = {}
             for s in range(PAIRS + 2):
                 if s + 2 < PAIRS:
@@ -203,15 +211,15 @@ def tile_feedforwardse3_pb_t_kernel(tc, x, w_in, scale, bias, w_out, out):
                 if s >= 2:
                     take_root(s - 2)
 
-        with tc.tile_pool(name="gate", bufs=3) as gate_pool, tc.tile_pool(
+        with tc.tile_pool(name="gate", bufs=2) as gate_pool, tc.tile_pool(
             name="g", bufs=2
         ) as g_pool, tc.tile_pool(name="result", bufs=3) as result_pool, tc.psum_pool(name="h", bufs=4) as h_pool, tc.psum_pool(
             name="y", bufs=4
         ) as y_pool:
 
-            def gate(q):
-                cols = slice(q * PAIR, (q + 1) * PAIR)
-                gelu = gate_pool.tile([P, PACK, PAIR], F32)
+            def gate(c):
+                cols = slice(c * CHUNK, (c + 1) * CHUNK)
+                gelu = gate_pool.tile([P, PACK, CHUNK], F32)
                 for j in range(PACK):
                     nc.scalar.activation(
                         out=gelu[:, j, :],
@@ -220,7 +228,7 @@ def tile_feedforwardse3_pb_t_kernel(tc, x, w_in, scale, bias, w_out, out):
                         scale=scale_f32[:, j : j + 1],
                         bias=bias_f32[:, j : j + 1],
                     )
-                factor = gate_pool.tile([P, PAIR, PACK], F32)
+                factor = gate_pool.tile([P, CHUNK, PACK], F32)
                 nc.vector.tensor_mul(
                     out=factor[:],
                     in0=gelu[:].rearrange("p j t -> p t j"),
@@ -255,7 +263,7 @@ def tile_feedforwardse3_pb_t_kernel(tc, x, w_in, scale, bias, w_out, out):
                     nc.vector.tensor_tensor(
                         out=g_grouped[:, m],
                         in0=h[:].rearrange("p j t -> p t j"),
-                        in1=factor[:, (i % 2) * P : (i % 2 + 1) * P, :],
+                        in1=factor[:, (i * P) % CHUNK : (i * P) % CHUNK + P, :],
                         op=ALU.mult,
                     )
                     if m > 0:
@@ -282,16 +290,22 @@ def tile_feedforwardse3_pb_t_kernel(tc, x, w_in, scale, bias, w_out, out):
                         out=result[:, b * KEEP : b * KEEP + kept, :],
                         in_=y[:, 0 : M2 * KEEP].rearrange("p (m d) -> p d m", m=M2)[:, 0:kept, :],
                     )
-                nc.sync.dma_start(
-                    out=out_rows[i * P : (i + 1) * P, :], in_=result[:].rearrange("p d m -> p (d m)")
-                )
+                    if b % 3 == 2:
+                        done = slice((b - 2) * KEEP, b * KEEP + kept)
+                        nc.sync.dma_start(
+                            out=out_rows[i * P : (i + 1) * P, :].rearrange("t (d m) -> t d m", m=M2)[
+                                :, done, :
+                            ],
+                            in_=result[:, done, :],
+                        )
 
             factors = {0: gate(0)}
             g_of = {}
             for i in range(TILES + 1):
                 if i < TILES:
-                    g_of[i] = hidden(i, factors[i // 2])
-                    if i % 2 == 0 and i // 2 + 1 < PAIRS:
-                        factors[i // 2 + 1] = gate(i // 2 + 1)
+                    c = i * P // CHUNK
+                    g_of[i] = hidden(i, factors[c])
+                    if i * P % CHUNK == 0 and c + 1 < CHUNKS:
+                        factors[c + 1] = gate(c + 1)
                 if i >= 1:
                     project(i - 1, g_of[i - 1][0], g_of[i - 1][1])

@@ -213,8 +213,8 @@ def tile_feedforwardse3_pb_t_kernel(tc, x, w_in, scale, bias, w_out, out):
 
         with tc.tile_pool(name="gate", bufs=2) as gate_pool, tc.tile_pool(
             name="g", bufs=2
-        ) as g_pool, tc.tile_pool(name="result", bufs=3) as result_pool, tc.psum_pool(name="h", bufs=4) as h_pool, tc.psum_pool(
-            name="y", bufs=4
+        ) as g_pool, tc.tile_pool(name="result", bufs=3) as result_pool, tc.psum_pool(name="h", bufs=5) as h_pool, tc.psum_pool(
+            name="y", bufs=3
         ) as y_pool:
 
             def gate(c):
@@ -228,11 +228,11 @@ def tile_feedforwardse3_pb_t_kernel(tc, x, w_in, scale, bias, w_out, out):
                         scale=scale_f32[:, j : j + 1],
                         bias=bias_f32[:, j : j + 1],
                     )
-                factor = gate_pool.tile([P, CHUNK, PACK], F32)
+                factor = gate_pool.tile([P, 2, CHUNK, 2], F32)
                 nc.vector.tensor_mul(
                     out=factor[:],
-                    in0=gelu[:].rearrange("p j t -> p t j"),
-                    in1=rnorm[:, :, cols].rearrange("p j t -> p t j"),
+                    in0=gelu[:].rearrange("p (a b) t -> p a t b", b=2),
+                    in1=rnorm[:, :, cols].rearrange("p (a b) t -> p a t b", b=2),
                 )
                 return factor
 
@@ -261,9 +261,11 @@ def tile_feedforwardse3_pb_t_kernel(tc, x, w_in, scale, bias, w_out, out):
                             stop=True,
                         )
                     nc.vector.tensor_tensor(
-                        out=g_grouped[:, m],
-                        in0=h[:].rearrange("p j t -> p t j"),
-                        in1=factor[:, (i * P) % CHUNK : (i * P) % CHUNK + P, :],
+                        out=g_grouped[:, m].rearrange("p t (a b) -> p t a b", b=2),
+                        in0=h[:].rearrange("p (a b) t -> p t a b", b=2),
+                        in1=factor[:, :, (i * P) % CHUNK : (i * P) % CHUNK + P, :].rearrange(
+                            "p a t b -> p t a b"
+                        ),
                         op=ALU.mult,
                     )
                     if m > 0:

@@ -39,6 +39,7 @@ def tile_feedforwardse3_pb_t_kernel(tc, x, w_in, scale, bias, w_out, out):
 
     with ExitStack() as ctx:
         resident = ctx.enter_context(tc.tile_pool(name="resident", bufs=1))
+        gate_pool = ctx.enter_context(tc.tile_pool(name="gate", bufs=2))
 
         ident = resident.tile([P, P], F32)
         make_identity(nc, ident[:])
@@ -56,7 +57,7 @@ def tile_feedforwardse3_pb_t_kernel(tc, x, w_in, scale, bias, w_out, out):
         bias_f32 = resident.tile([P, PACK], F32)
 
         with tc.tile_pool(name="weights", bufs=1) as weights, tc.tile_pool(
-            name="loaded", bufs=3
+            name="loaded", bufs=2
         ) as loaded_pool, tc.tile_pool(name="split", bufs=2) as split_pool, tc.tile_pool(
             name="grouped", bufs=4
         ) as grouped_pool, tc.tile_pool(name="squares", bufs=2) as square_pool, tc.psum_pool(
@@ -102,7 +103,7 @@ def tile_feedforwardse3_pb_t_kernel(tc, x, w_in, scale, bias, w_out, out):
                         for u in range(2):
                             nc.tensor.transpose(xt[:, a, u, :], words[:, a, m, u, :], ident[:])
                     grouped = grouped_pool.tile([P, PAIR, PACK], BF16, align_bytes=64)
-                    copy = nc.scalar.copy if m % 2 == 0 else nc.vector.tensor_copy
+                    copy = nc.scalar.copy if m % 2 == 1 else nc.vector.tensor_copy
                     copy(
                         out=grouped[:].bitcast(F32).rearrange("p (a t) u -> p a t u", a=2),
                         in_=xt[:].rearrange("p a u t -> p a t u"),
@@ -129,20 +130,24 @@ def tile_feedforwardse3_pb_t_kernel(tc, x, w_in, scale, bias, w_out, out):
                     sq = square_pool.tile([P, F], F32, name="sq%d" % m)
                     nc.scalar.activation(out=sq[:], in_=ht[:], func=ACT.Square)
                     squares.append(sq)
-                return squares
+                    if m % 2 == 1:
+                        nc.gpsimd.tensor_tensor(
+                            out=sq[:], in0=sq[:], in1=squares[m - 1][:], op=ALU.add
+                        )
+                return squares[1::2] + squares[M2 - 1 :]
 
             def sum_squares(i, squares):
                 cols = slice(i * P, (i + 1) * P)
                 sums = sum_pool.tile([P, PACK, P], F32)
                 for j in range(PACK):
-                    for m in range(M2):
+                    for n, plane in enumerate(squares):
                         nc.tensor.matmul(
                             out=sums[:, j, :],
-                            lhsT=squares[m][:, j * P : (j + 1) * P],
+                            lhsT=plane[:, j * P : (j + 1) * P],
                             rhs=ident[:],
                             is_transpose=True,
-                            start=(m == 0),
-                            stop=(m == M2 - 1),
+                            start=(n == 0),
+                            stop=(n == len(squares) - 1),
                         )
                 nc.vector.tensor_scalar_max(out=norm[:, :, cols], in0=sums[:], scalar1=EPS * EPS)
 
@@ -211,7 +216,7 @@ def tile_feedforwardse3_pb_t_kernel(tc, x, w_in, scale, bias, w_out, out):
                 if s >= 2:
                     take_root(s - 2)
 
-        with tc.tile_pool(name="gate", bufs=2) as gate_pool, tc.tile_pool(
+        with tc.tile_pool(
             name="g", bufs=2
         ) as g_pool, tc.tile_pool(name="result", bufs=3) as result_pool, tc.psum_pool(name="h", bufs=5) as h_pool, tc.psum_pool(
             name="y", bufs=3
@@ -219,7 +224,7 @@ def tile_feedforwardse3_pb_t_kernel(tc, x, w_in, scale, bias, w_out, out):
 
             def gate(c):
                 cols = slice(c * CHUNK, (c + 1) * CHUNK)
-                gelu = gate_pool.tile([P, PACK, CHUNK], F32)
+                gelu = gate_pool.tile([P, PACK, CHUNK], F32, bufs=1)
                 for j in range(PACK):
                     nc.scalar.activation(
                         out=gelu[:, j, :],
@@ -301,13 +306,13 @@ def tile_feedforwardse3_pb_t_kernel(tc, x, w_in, scale, bias, w_out, out):
                             in_=result[:, done, :],
                         )
 
-            factors = {0: gate(0)}
+            factors = {0: gate(0), 1: gate(1)}
             g_of = {}
             for i in range(TILES + 1):
                 if i < TILES:
                     c = i * P // CHUNK
                     g_of[i] = hidden(i, factors[c])
-                    if i * P % CHUNK == 0 and c + 1 < CHUNKS:
-                        factors[c + 1] = gate(c + 1)
+                    if (i + 1) * P % CHUNK == 0 and c + 2 < CHUNKS:
+                        factors[c + 2] = gate(c + 2)
                 if i >= 1:
                     project(i - 1, g_of[i - 1][0], g_of[i - 1][1])

@@ -38,6 +38,7 @@ def tile_feedforwardse3_pb_t_kernel(tc, x, w_in, scale, bias, w_out, out):
     out_rows = out.rearrange("b n d m -> (b n) (d m)")
 
     with ExitStack() as ctx:
+        ctx.enter_context(tc.manual_schedule())
         resident = ctx.enter_context(tc.tile_pool(name="resident", bufs=1))
         gate_pool = ctx.enter_context(tc.tile_pool(name="gate", bufs=2))
 
@@ -61,30 +62,25 @@ def tile_feedforwardse3_pb_t_kernel(tc, x, w_in, scale, bias, w_out, out):
         ) as loaded_pool, tc.tile_pool(name="split", bufs=2) as split_pool, tc.tile_pool(
             name="grouped", bufs=4
         ) as grouped_pool, tc.tile_pool(name="squares", bufs=2) as square_pool, tc.psum_pool(
-            name="xt", bufs=3
+            name="xt", bufs=2
         ) as xt_pool, tc.psum_pool(name="ht", bufs=4) as ht_pool, tc.psum_pool(
-            name="sums", bufs=1
+            name="sums", bufs=2
         ) as sum_pool:
 
             def load_pair(q):
                 x_sb = loaded_pool.tile([P, 2, ROW], BF16)
-                nc.sync.dma_start(
-                    out=x_sb[:],
-                    in_=x_rows[q * PAIR : (q + 1) * PAIR, :].rearrange("(a p) c -> p a c", p=P),
-                )
+                for a in range(2):
+                    rows = slice(q * PAIR + a * P, q * PAIR + (a + 1) * P)
+                    nc.sync.dma_start(out=x_sb[:, a, :], in_=x_rows[rows, :])
                 return x_sb
 
-            def split_components(x_sb):
-                x_split = split_pool.tile([P, 2, M2, D], BF16)
-                for a in range(2):
-                    for planes in (slice(0, 3), slice(3, M2)):
-                        nc.vector.tensor_copy(
-                            out=x_split[:, a, planes, :].rearrange("p m (c i) -> p c m i", i=PACK),
-                            in_=x_sb[:, a, :].rearrange("p (c i m) -> p c m i", i=PACK, m=M2)[
-                                :, :, planes, :
-                            ],
-                        )
-                return x_split
+            def split_half(x_sb, x_split, a, planes):
+                nc.vector.tensor_copy(
+                    out=x_split[:, a, planes, :].rearrange("p m (c i) -> p c m i", i=PACK),
+                    in_=x_sb[:, a, :].rearrange("p (c i m) -> p c m i", i=PACK, m=M2)[
+                        :, :, planes, :
+                    ],
+                )
 
             def quantise_x(q, m, grouped):
                 cols = slice(q * PAIR, (q + 1) * PAIR)
@@ -94,24 +90,21 @@ def tile_feedforwardse3_pb_t_kernel(tc, x, w_in, scale, bias, w_out, out):
                     in_=grouped[:].rearrange("p t i -> p (t i)"),
                 )
 
-            def pack_pair(q, x_split):
+            def transpose_x(x_split, m):
                 words = x_split[:].bitcast(F32).rearrange("p a m (u q) -> p a m u q", u=2)
-                groups = []
-                for m in range(M2):
-                    xt = xt_pool.tile([P, 2, 2, P], F32)
-                    for a in range(2):
-                        for u in range(2):
-                            nc.tensor.transpose(xt[:, a, u, :], words[:, a, m, u, :], ident[:])
-                    grouped = grouped_pool.tile([P, PAIR, PACK], BF16, align_bytes=64)
-                    copy = nc.scalar.copy if m % 2 == 1 else nc.vector.tensor_copy
-                    copy(
-                        out=grouped[:].bitcast(F32).rearrange("p (a t) u -> p a t u", a=2),
-                        in_=xt[:].rearrange("p a u t -> p a t u"),
-                    )
-                    groups.append(grouped)
-                    if m > 0:
-                        quantise_x(q, m - 1, groups[m - 1])
-                quantise_x(q, M2 - 1, groups[M2 - 1])
+                xt = xt_pool.tile([P, 2, 2, P], F32)
+                for a in range(2):
+                    for u in range(2):
+                        nc.tensor.transpose(xt[:, a, u, :], words[:, a, m, u, :], ident[:])
+                return xt
+
+            def group_x(xt, copy):
+                grouped = grouped_pool.tile([P, PAIR, PACK], BF16, align_bytes=64)
+                copy(
+                    out=grouped[:].bitcast(F32).rearrange("p (a t) u -> p a t u", a=2),
+                    in_=xt[:].rearrange("p a u t -> p a t u"),
+                )
+                return grouped
 
             def square_h(i):
                 cols = slice(i * P, (i + 1) * P)
@@ -130,14 +123,9 @@ def tile_feedforwardse3_pb_t_kernel(tc, x, w_in, scale, bias, w_out, out):
                     sq = square_pool.tile([P, F], F32, name="sq%d" % m)
                     nc.scalar.activation(out=sq[:], in_=ht[:], func=ACT.Square)
                     squares.append(sq)
-                    if m % 2 == 1:
-                        nc.gpsimd.tensor_tensor(
-                            out=sq[:], in0=sq[:], in1=squares[m - 1][:], op=ALU.add
-                        )
-                return squares[1::2] + squares[M2 - 1 :]
+                return squares
 
-            def sum_squares(i, squares):
-                cols = slice(i * P, (i + 1) * P)
+            def sum_squares(squares):
                 sums = sum_pool.tile([P, PACK, P], F32)
                 for j in range(PACK):
                     for n, plane in enumerate(squares):
@@ -149,15 +137,22 @@ def tile_feedforwardse3_pb_t_kernel(tc, x, w_in, scale, bias, w_out, out):
                             start=(n == 0),
                             stop=(n == len(squares) - 1),
                         )
-                nc.vector.tensor_scalar_max(out=norm[:, :, cols], in0=sums[:], scalar1=EPS * EPS)
+                return sums
 
-            def take_root(q):
-                cols = slice(q * PAIR, (q + 1) * PAIR)
+            def take_root(i, sums):
+                cols = slice(i * P, (i + 1) * P)
                 nc.scalar.activation(
-                    out=rnorm[:, :, cols], in_=norm[:, :, cols], func=ACT.Abs_reciprocal_sqrt
+                    out=rnorm[:, :, cols], in_=sums[:], func=ACT.Abs_reciprocal_sqrt
                 )
-                nc.vector.tensor_mul(
-                    out=norm[:, :, cols], in0=norm[:, :, cols], in1=rnorm[:, :, cols]
+            def take_norm(i, sums):
+                cols = slice(i * P, (i + 1) * P)
+                nc.vector.scalar_tensor_tensor(
+                    out=norm[:, :, cols],
+                    in0=rnorm[:, :, cols],
+                    scalar=1.0 / EPS,
+                    in1=sums[:],
+                    op0=ALU.min,
+                    op1=ALU.mult,
                 )
 
             loaded = {0: load_pair(0)}
@@ -175,17 +170,20 @@ def tile_feedforwardse3_pb_t_kernel(tc, x, w_in, scale, bias, w_out, out):
             nc.sync.dma_start(out=bias_raw[:], in_=bias.rearrange("a b (p j) -> (a b p) j", j=PACK))
             nc.gpsimd.tensor_copy(out=scale_f32[:], in_=scale_raw[:])
             nc.gpsimd.tensor_copy(out=bias_f32[:], in_=bias_raw[:])
-            split = {0: split_components(loaded[0])}
+            halves = [(a, planes) for a in range(2) for planes in (slice(0, 3), slice(3, M2))]
+            split = {0: split_pool.tile([P, 2, M2, D], BF16, name="x_split")}
+            for a, planes in halves:
+                split_half(loaded[0], split[0], a, planes)
 
             w_in_grouped = weights.tile([P, PACK, P, PACK], BF16, align_bytes=64)
-            nc.vector.tensor_copy(
+            nc.scalar.copy(
                 out=w_in_grouped[:], in_=w_in_raw[:].rearrange("p i (q j) -> p j q i", j=PACK)
             )
             w_out_grouped = weights.tile([P, BLOCKS, WINDOW, PACK], BF16, align_bytes=64)
-            nc.vector.memset(w_out_grouped[:, BLOCKS - 1], 0.0)
+            nc.gpsimd.memset(w_out_grouped[:, BLOCKS - 1], 0.0)
             for b in range(BLOCKS):
                 width = min(WINDOW, D - b * KEEP)
-                nc.vector.tensor_copy(
+                nc.scalar.copy(
                     out=w_out_grouped[:, b, 0:width, :],
                     in_=w_out_raw[:, :, b * KEEP : b * KEEP + width].rearrange("p j d -> p d j"),
                 )
@@ -202,19 +200,42 @@ def tile_feedforwardse3_pb_t_kernel(tc, x, w_in, scale, bias, w_out, out):
                 )
             squares = {}
             for s in range(PAIRS + 2):
+                packs = s < PAIRS
                 if s + 2 < PAIRS:
                     loaded[s + 2] = load_pair(s + 2)
-                if s < PAIRS:
-                    pack_pair(s, split[s])
                 if s + 1 < PAIRS:
-                    split[s + 1] = split_components(loaded[s + 1])
-                for i in (2 * (s - 1), 2 * (s - 1) + 1):
+                    split[s + 1] = split_pool.tile([P, 2, M2, D], BF16, name="x_split")
+                xt = {}
+                groups = {}
+                for half in range(2):
+                    i = 2 * (s - 1) + half
+                    k = i - 2
+                    ms = (2 * half, 2 * half + 1) + ((4,) if half else ())
+                    if packs:
+                        xt[ms[0]] = transpose_x(split[s], ms[0])
+                    if 0 <= k < TILES:
+                        sums = sum_squares(squares[k])
+                        take_root(k, sums)
+                    if packs:
+                        for m in ms[1:]:
+                            xt[m] = transpose_x(split[s], m)
+                        groups[ms[0]] = group_x(xt[ms[0]], nc.vector.tensor_copy)
+                        groups[ms[1]] = group_x(xt[ms[1]], nc.scalar.copy)
+                    if s + 1 < PAIRS:
+                        split_half(loaded[s + 1], split[s + 1], *halves[2 * half])
+                    if 0 <= k < TILES:
+                        take_norm(k, sums)
                     if 0 <= i < TILES:
                         squares[i] = square_h(i)
-                    if 0 <= i - 1 < TILES:
-                        sum_squares(i - 1, squares[i - 1])
-                if s >= 2:
-                    take_root(s - 2)
+                    if packs:
+                        if half:
+                            groups[4] = group_x(xt[4], nc.vector.tensor_copy)
+                        quantise_x(s, ms[0], groups[ms[0]])
+                    if s + 1 < PAIRS:
+                        split_half(loaded[s + 1], split[s + 1], *halves[2 * half + 1])
+                    if packs:
+                        for m in ms[1:]:
+                            quantise_x(s, m, groups[m])
 
         with tc.tile_pool(
             name="g", bufs=2
@@ -234,11 +255,16 @@ def tile_feedforwardse3_pb_t_kernel(tc, x, w_in, scale, bias, w_out, out):
                         bias=bias_f32[:, j : j + 1],
                     )
                 factor = gate_pool.tile([P, 2, CHUNK, 2], F32)
-                nc.vector.tensor_mul(
-                    out=factor[:],
-                    in0=gelu[:].rearrange("p (a b) t -> p a t b", b=2),
-                    in1=rnorm[:, :, cols].rearrange("p (a b) t -> p a t b", b=2),
-                )
+                for a in range(2):
+                    pair = slice(2 * a, 2 * a + 2)
+                    nc.vector.scalar_tensor_tensor(
+                        out=factor[:, a],
+                        in0=rnorm[:, pair, cols].rearrange("p b t -> p t b"),
+                        scalar=1.0 / EPS,
+                        in1=gelu[:, pair, :].rearrange("p b t -> p t b"),
+                        op0=ALU.min,
+                        op1=ALU.mult,
+                    )
                 return factor
 
             def quantise_g(m, g_grouped, g_codes, g_scales):

@@ -21,10 +21,6 @@ ROW = D * M2
 EPS = 1e-12
 
 TILES = TOKENS // P
-PAIR = 2 * P
-PAIRS = TOKENS // PAIR
-CHUNK = 4 * P
-CHUNKS = TOKENS // CHUNK
 WINDOW = 128
 KEEP = 96
 BLOCKS = -(-D // KEEP)
@@ -41,6 +37,10 @@ def tile_feedforwardse3_pb_t_kernel(tc, x, w_in, scale, bias, w_out, out):
         ctx.enter_context(tc.manual_schedule())
         resident = ctx.enter_context(tc.tile_pool(name="resident", bufs=1))
         gate_pool = ctx.enter_context(tc.tile_pool(name="gate", bufs=2))
+        square_pool = ctx.enter_context(tc.tile_pool(name="squares", bufs=2))
+        wide_pool = ctx.enter_context(tc.psum_pool(name="wide", bufs=4))
+        even_pool = ctx.enter_context(tc.psum_pool(name="even", bufs=2))
+        odd_pool = ctx.enter_context(tc.psum_pool(name="odd", bufs=2))
 
         ident = resident.tile([P, P], F32)
         make_identity(nc, ident[:])
@@ -49,131 +49,156 @@ def tile_feedforwardse3_pb_t_kernel(tc, x, w_in, scale, bias, w_out, out):
         w_in_scales = resident.tile([P, F], U8, align_bytes=64)
         w_out_codes = resident.tile([P, BLOCKS, WINDOW], U32, align_bytes=64)
         w_out_scales = resident.tile([P, BLOCKS, WINDOW], U8, align_bytes=64)
-        x_codes = resident.tile([P, M2, TOKENS], U32, align_bytes=64)
-        x_scales = resident.tile([P, M2, TOKENS], U8, align_bytes=64)
+        x_codes = resident.tile([P, TILES, M2, P], U32, align_bytes=64)
+        x_scales = resident.tile([P, TILES, M2, P], U8, align_bytes=64)
 
         norm = resident.tile([P, PACK, TOKENS], F32)
         rnorm = resident.tile([P, PACK, TOKENS], F32)
         scale_f32 = resident.tile([P, PACK], F32)
         bias_f32 = resident.tile([P, PACK], F32)
 
+        squares = {}
+        sums = {}
+
+        def multiply_and_square(i, ms):
+            for m in ms:
+                ht = wide_pool.tile([P, F], F32, name="wide")
+                nc.tensor.matmul_mx(
+                    out=ht[:],
+                    lhsT=x_codes[:, i, m, :].bitcast(FP8X4),
+                    lhsT_scale=x_scales[:, i, m, :],
+                    rhs=w_in_codes[:].bitcast(FP8X4),
+                    rhs_scale=w_in_scales[:],
+                    start=True,
+                    stop=True,
+                )
+                sq = square_pool.tile([P, F], F32, name="sq%d" % m)
+                nc.scalar.activation(out=sq[:], in_=ht[:], func=ACT.Square)
+                squares[i, m] = sq
+
+        def add_squares(i, m, n, eng):
+            eng.tensor_tensor(
+                out=squares[i, m][:], in0=squares[i, m][:], in1=squares[i, n][:], op=ALU.add
+            )
+
+        def sum_squares(i, js, planes):
+            if js[0] == 0:
+                sums[i] = odd_pool.tile([P, PACK, P], F32, name="odd")
+            for j in js:
+                for n, m in enumerate(planes):
+                    nc.tensor.matmul(
+                        out=sums[i][:, j, :],
+                        lhsT=squares[i, m][:, j * P : (j + 1) * P],
+                        rhs=ident[:],
+                        is_transpose=True,
+                        start=(n == 0),
+                        stop=(n == len(planes) - 1),
+                    )
+
+        def take_root(i):
+            cols = slice(i * P, (i + 1) * P)
+            nc.scalar.activation(
+                out=rnorm[:, :, cols], in_=sums[i][:], func=ACT.Abs_reciprocal_sqrt
+            )
+
+        def take_norm(i):
+            cols = slice(i * P, (i + 1) * P)
+            nc.vector.scalar_tensor_tensor(
+                out=norm[:, :, cols],
+                in0=rnorm[:, :, cols],
+                scalar=1.0 / EPS,
+                in1=sums[i][:],
+                op0=ALU.min,
+                op1=ALU.mult,
+            )
+
+        ADDS = lambda i: 0
+        planes = {0: (0, 1, 2, 3, 4), 1: (1, 2, 3, 4), 2: (1, 3, 4), 4: (4,)}
+
+        def p1_step(h, front=lambda n: None):
+            i, k = h - 1, h - 3
+            adds = 0 <= i < TILES and ADDS(i) or 0
+            front(0)
+            for st in ("sa", 1, "ma", "sb", "r", 2, "n", "mb", 3):
+                if isinstance(st, int):
+                    front(st)
+                elif st == "sa" and 0 <= k < TILES:
+                    sum_squares(k, (0, 1), planes[ADDS(k)])
+                elif st == "sb" and 0 <= k < TILES:
+                    sum_squares(k, (2, 3), planes[ADDS(k)])
+                elif st == "r" and 0 <= k < TILES:
+                    take_root(k)
+                elif st == "n" and 0 <= k < TILES:
+                    take_norm(k)
+                elif st == "ma" and 0 <= i < TILES:
+                    multiply_and_square(i, (0, 1))
+                    if adds > 0:
+                        add_squares(i, 1, 0, nc.gpsimd if adds < 4 else nc.vector)
+                elif st == "mb" and 0 <= i < TILES:
+                    multiply_and_square(i, (2, 3, 4))
+                    if adds == 2:
+                        add_squares(i, 3, 2, nc.gpsimd)
+                    if adds == 4:
+                        add_squares(i, 2, 1, nc.vector)
+                        add_squares(i, 3, 2, nc.vector)
+                        add_squares(i, 4, 3, nc.vector)
+
         with tc.tile_pool(name="weights", bufs=1) as weights, tc.tile_pool(
-            name="loaded", bufs=2
+            name="loaded", bufs=4
         ) as loaded_pool, tc.tile_pool(name="split", bufs=2) as split_pool, tc.tile_pool(
             name="grouped", bufs=4
-        ) as grouped_pool, tc.tile_pool(name="squares", bufs=2) as square_pool, tc.psum_pool(
-            name="xt", bufs=2
-        ) as xt_pool, tc.psum_pool(name="ht", bufs=4) as ht_pool, tc.psum_pool(
-            name="sums", bufs=2
-        ) as sum_pool:
+        ) as grouped_pool:
+            loaded = {}
+            split = {}
+            xt = {}
+            grouped = {}
 
-            def load_pair(q):
-                x_sb = loaded_pool.tile([P, 2, ROW], BF16)
-                for a in range(2):
-                    rows = slice(q * PAIR + a * P, q * PAIR + (a + 1) * P)
-                    nc.sync.dma_start(out=x_sb[:, a, :], in_=x_rows[rows, :])
-                return x_sb
+            def load_tile(i):
+                loaded[i] = loaded_pool.tile([P, ROW], BF16, name="x_sb")
+                nc.sync.dma_start(out=loaded[i][:], in_=x_rows[i * P : (i + 1) * P, :])
 
-            def split_half(x_sb, x_split, a, planes):
+            def split_part(i, ms):
+                if ms.start == 0:
+                    split[i] = split_pool.tile([P, M2, D], BF16, name="x_split")
                 nc.vector.tensor_copy(
-                    out=x_split[:, a, planes, :].rearrange("p m (c i) -> p c m i", i=PACK),
-                    in_=x_sb[:, a, :].rearrange("p (c i m) -> p c m i", i=PACK, m=M2)[
-                        :, :, planes, :
-                    ],
+                    out=split[i][:, ms, :].rearrange("p m (c i) -> p c m i", i=PACK),
+                    in_=loaded[i][:].rearrange("p (c i m) -> p c m i", i=PACK, m=M2)[:, :, ms, :],
                 )
 
-            def quantise_x(q, m, grouped):
-                cols = slice(q * PAIR, (q + 1) * PAIR)
-                nc.vector.quantize_mx(
-                    out=x_codes[:, m, cols].bitcast(FP8X4),
-                    scales=x_scales[:, m, cols],
-                    in_=grouped[:].rearrange("p t i -> p (t i)"),
-                )
-
-            def transpose_x(x_split, m):
-                words = x_split[:].bitcast(F32).rearrange("p a m (u q) -> p a m u q", u=2)
-                xt = xt_pool.tile([P, 2, 2, P], F32)
-                for a in range(2):
+            def transpose_x(i, ms):
+                words = split[i][:].bitcast(F32).rearrange("p m (u q) -> p m u q", u=2)
+                xt[i, ms] = even_pool.tile([P, len(ms), 2, P], F32, name="even")
+                for n, m in enumerate(ms):
                     for u in range(2):
-                        nc.tensor.transpose(xt[:, a, u, :], words[:, a, m, u, :], ident[:])
-                return xt
+                        nc.tensor.transpose(xt[i, ms][:, n, u, :], words[:, m, u, :], ident[:])
 
-            def group_x(xt, copy):
-                grouped = grouped_pool.tile([P, PAIR, PACK], BF16, align_bytes=64)
+            def group_x(i, ms, copy):
+                grouped[i, ms] = grouped_pool.tile([P, len(ms), P, PACK], BF16, align_bytes=64, name="grouped%d" % len(ms))
                 copy(
-                    out=grouped[:].bitcast(F32).rearrange("p (a t) u -> p a t u", a=2),
-                    in_=xt[:].rearrange("p a u t -> p a t u"),
-                )
-                return grouped
-
-            def square_h(i):
-                cols = slice(i * P, (i + 1) * P)
-                squares = []
-                for m in range(M2):
-                    ht = ht_pool.tile([P, F], F32)
-                    nc.tensor.matmul_mx(
-                        out=ht[:],
-                        lhsT=x_codes[:, m, cols].bitcast(FP8X4),
-                        lhsT_scale=x_scales[:, m, cols],
-                        rhs=w_in_codes[:].bitcast(FP8X4),
-                        rhs_scale=w_in_scales[:],
-                        start=True,
-                        stop=True,
-                    )
-                    sq = square_pool.tile([P, F], F32, name="sq%d" % m)
-                    nc.scalar.activation(out=sq[:], in_=ht[:], func=ACT.Square)
-                    squares.append(sq)
-                return squares
-
-            def sum_squares(squares):
-                sums = sum_pool.tile([P, PACK, P], F32)
-                for j in range(PACK):
-                    for n, plane in enumerate(squares):
-                        nc.tensor.matmul(
-                            out=sums[:, j, :],
-                            lhsT=plane[:, j * P : (j + 1) * P],
-                            rhs=ident[:],
-                            is_transpose=True,
-                            start=(n == 0),
-                            stop=(n == len(squares) - 1),
-                        )
-                return sums
-
-            def take_root(i, sums):
-                cols = slice(i * P, (i + 1) * P)
-                nc.scalar.activation(
-                    out=rnorm[:, :, cols], in_=sums[:], func=ACT.Abs_reciprocal_sqrt
-                )
-            def take_norm(i, sums):
-                cols = slice(i * P, (i + 1) * P)
-                nc.vector.scalar_tensor_tensor(
-                    out=norm[:, :, cols],
-                    in0=rnorm[:, :, cols],
-                    scalar=1.0 / EPS,
-                    in1=sums[:],
-                    op0=ALU.min,
-                    op1=ALU.mult,
+                    out=grouped[i, ms][:].rearrange("p m t i -> p m (t i)").bitcast(F32).rearrange("p m (t u) -> p m t u", u=2),
+                    in_=xt[i, ms][:].rearrange("p m u t -> p m t u"),
                 )
 
-            loaded = {0: load_pair(0)}
+            def quantise_x(i, ms):
+                nc.vector.quantize_mx(
+                    out=x_codes[:, i, ms[0] : ms[-1] + 1, :].rearrange("p m t -> p (m t)").bitcast(FP8X4),
+                    scales=x_scales[:, i, ms[0] : ms[-1] + 1, :].rearrange("p m t -> p (m t)"),
+                    in_=grouped[i, ms][:].rearrange("p m t i -> p (m t i)"),
+                )
+
+            load_tile(0)
             w_in_raw = weights.tile([P, PACK, F], BF16)
             nc.sync.dma_start(
                 out=w_in_raw[:].rearrange("p (u e) f -> p u e f", u=2),
                 in_=w_in.rearrange("(u p e) f -> p u e f", u=2, e=2),
             )
-            loaded[1] = load_pair(1)
-            w_out_raw = weights.tile([P, PACK, D], BF16)
-            nc.sync.dma_start(out=w_out_raw[:], in_=w_out.rearrange("(p j) d -> p j d", j=PACK))
+            load_tile(1)
+            load_tile(2)
+            load_tile(3)
             scale_raw = weights.tile([P, PACK], BF16)
             nc.sync.dma_start(out=scale_raw[:], in_=scale.rearrange("a b (p j) -> (a b p) j", j=PACK))
             bias_raw = weights.tile([P, PACK], BF16)
             nc.sync.dma_start(out=bias_raw[:], in_=bias.rearrange("a b (p j) -> (a b p) j", j=PACK))
-            nc.gpsimd.tensor_copy(out=scale_f32[:], in_=scale_raw[:])
-            nc.gpsimd.tensor_copy(out=bias_f32[:], in_=bias_raw[:])
-            halves = [(a, planes) for a in range(2) for planes in (slice(0, 3), slice(3, M2))]
-            split = {0: split_pool.tile([P, 2, M2, D], BF16, name="x_split")}
-            for a, planes in halves:
-                split_half(loaded[0], split[0], a, planes)
 
             w_in_grouped = weights.tile([P, PACK, P, PACK], BF16, align_bytes=64)
             nc.scalar.copy(
@@ -181,164 +206,195 @@ def tile_feedforwardse3_pb_t_kernel(tc, x, w_in, scale, bias, w_out, out):
             )
             w_out_grouped = weights.tile([P, BLOCKS, WINDOW, PACK], BF16, align_bytes=64)
             nc.gpsimd.memset(w_out_grouped[:, BLOCKS - 1], 0.0)
-            for b in range(BLOCKS):
+            nc.gpsimd.tensor_copy(out=scale_f32[:], in_=scale_raw[:])
+            nc.gpsimd.tensor_copy(out=bias_f32[:], in_=bias_raw[:])
+
+            def w_out_group(b, w_out_raw):
                 width = min(WINDOW, D - b * KEEP)
-                nc.scalar.copy(
+                nc.gpsimd.tensor_scalar(
                     out=w_out_grouped[:, b, 0:width, :],
-                    in_=w_out_raw[:, :, b * KEEP : b * KEEP + width].rearrange("p j d -> p d j"),
+                    in0=w_out_raw[:, :, b * KEEP : b * KEEP + width].rearrange("p j d -> p d j"),
+                    scalar1=1.0,
+                    scalar2=0.0,
+                    op0=ALU.mult,
+                    op1=ALU.add,
                 )
-            nc.vector.quantize_mx(
-                out=w_in_codes[:].bitcast(FP8X4),
-                scales=w_in_scales[:],
-                in_=w_in_grouped[:].rearrange("p j q i -> p (j q i)"),
-            )
-            for b in range(BLOCKS):
+
+            def w_out_quantise(b):
                 nc.vector.quantize_mx(
                     out=w_out_codes[:, b, :].bitcast(FP8X4),
                     scales=w_out_scales[:, b, :],
                     in_=w_out_grouped[:, b].rearrange("p d j -> p (d j)"),
                 )
-            squares = {}
-            for s in range(PAIRS + 2):
-                packs = s < PAIRS
-                if s + 2 < PAIRS:
-                    loaded[s + 2] = load_pair(s + 2)
-                if s + 1 < PAIRS:
-                    split[s + 1] = split_pool.tile([P, 2, M2, D], BF16, name="x_split")
-                xt = {}
-                groups = {}
-                for half in range(2):
-                    i = 2 * (s - 1) + half
-                    k = i - 2
-                    ms = (2 * half, 2 * half + 1) + ((4,) if half else ())
-                    if packs:
-                        xt[ms[0]] = transpose_x(split[s], ms[0])
-                    if 0 <= k < TILES:
-                        sums = sum_squares(squares[k])
-                        take_root(k, sums)
-                    if packs:
-                        for m in ms[1:]:
-                            xt[m] = transpose_x(split[s], m)
-                        groups[ms[0]] = group_x(xt[ms[0]], nc.vector.tensor_copy)
-                        groups[ms[1]] = group_x(xt[ms[1]], nc.scalar.copy)
-                    if s + 1 < PAIRS:
-                        split_half(loaded[s + 1], split[s + 1], *halves[2 * half])
-                    if 0 <= k < TILES:
-                        take_norm(k, sums)
-                    if 0 <= i < TILES:
-                        squares[i] = square_h(i)
-                    if packs:
-                        if half:
-                            groups[4] = group_x(xt[4], nc.vector.tensor_copy)
-                        quantise_x(s, ms[0], groups[ms[0]])
-                    if s + 1 < PAIRS:
-                        split_half(loaded[s + 1], split[s + 1], *halves[2 * half + 1])
-                    if packs:
-                        for m in ms[1:]:
-                            quantise_x(s, m, groups[m])
 
-        with tc.tile_pool(
-            name="g", bufs=2
-        ) as g_pool, tc.tile_pool(name="result", bufs=3) as result_pool, tc.psum_pool(name="h", bufs=5) as h_pool, tc.psum_pool(
-            name="y", bufs=3
-        ) as y_pool:
+            A, B, C = (0, 1), (2, 3), (4,)
+            for ms in (slice(0, 3), slice(3, M2)):
+                split_part(0, ms)
 
-            def gate(c):
-                cols = slice(c * CHUNK, (c + 1) * CHUNK)
-                gelu = gate_pool.tile([P, PACK, CHUNK], F32, bufs=1)
-                for j in range(PACK):
-                    nc.scalar.activation(
-                        out=gelu[:, j, :],
-                        in_=norm[:, j, cols],
-                        func=ACT.Gelu,
-                        scale=scale_f32[:, j : j + 1],
-                        bias=bias_f32[:, j : j + 1],
+            for h in range(TILES):
+                if h + 4 < TILES:
+                    load_tile(h + 4)
+                if h == 2:
+                    w_out_raw = weights.tile([P, PACK, D], BF16)
+                    nc.sync.dma_start(
+                        out=w_out_raw[:], in_=w_out.rearrange("(p j) d -> p j d", j=PACK)
                     )
-                factor = gate_pool.tile([P, 2, CHUNK, 2], F32)
-                for a in range(2):
-                    pair = slice(2 * a, 2 * a + 2)
-                    nc.vector.scalar_tensor_tensor(
-                        out=factor[:, a],
-                        in0=rnorm[:, pair, cols].rearrange("p b t -> p t b"),
-                        scalar=1.0 / EPS,
-                        in1=gelu[:, pair, :].rearrange("p b t -> p t b"),
-                        op0=ALU.min,
-                        op1=ALU.mult,
-                    )
-                return factor
 
-            def quantise_g(m, g_grouped, g_codes, g_scales):
-                nc.vector.quantize_mx(
-                    out=g_codes[:, m, :].bitcast(FP8X4),
-                    scales=g_scales[:, m, :],
-                    in_=g_grouped[:, m].rearrange("p t j -> p (t j)"),
+                def front(n):
+                    if n == 1:
+                        transpose_x(h, A)
+                        group_x(h, A, nc.vector.tensor_copy)
+                        if h + 1 < TILES:
+                            split_part(h + 1, slice(0, 3))
+                        quantise_x(h, A)
+                    if n == 2:
+                        transpose_x(h, B)
+                        group_x(h, B, nc.scalar.copy)
+                        transpose_x(h, C)
+                        group_x(h, C, nc.vector.tensor_copy)
+                        if h == 0:
+                            nc.vector.quantize_mx(
+                                out=w_in_codes[:].bitcast(FP8X4),
+                                scales=w_in_scales[:],
+                                in_=w_in_grouped[:].rearrange("p j q i -> p (j q i)"),
+                            )
+                    if n == 3:
+                        if h + 1 < TILES:
+                            split_part(h + 1, slice(3, M2))
+                        if 4 <= h < 4 + BLOCKS:
+                            w_out_group(h - 4, w_out_raw)
+                        if 5 <= h < 5 + BLOCKS:
+                            w_out_quantise(h - 5)
+                        quantise_x(h, B)
+                        quantise_x(h, C)
+
+                p1_step(h, front)
+
+        g_pool = ctx.enter_context(tc.tile_pool(name="g", bufs=2))
+        result_pool = ctx.enter_context(tc.tile_pool(name="result", bufs=3))
+        gelus = {}
+        factors = {}
+        g_of = {}
+        h_of = {}
+
+        def take_gelu(i):
+            cols = slice(i * P, (i + 1) * P)
+            gelus[i] = gate_pool.tile([P, PACK, P], F32, name="gelu")
+            for j in range(PACK):
+                nc.scalar.activation(
+                    out=gelus[i][:, j, :],
+                    in_=norm[:, j, cols],
+                    func=ACT.Gelu,
+                    scale=scale_f32[:, j : j + 1],
+                    bias=bias_f32[:, j : j + 1],
                 )
 
-            def hidden(i, factor):
-                cols = slice(i * P, (i + 1) * P)
-                g_grouped = g_pool.tile([P, M2, P, PACK], BF16, align_bytes=64)
-                g_codes = g_pool.tile([P, M2, P], U32, align_bytes=64)
-                g_scales = g_pool.tile([P, M2, P], U8, align_bytes=64)
-                for m in range(M2):
-                    h = h_pool.tile([P, PACK, P], F32)
-                    for j in range(PACK):
-                        nc.tensor.matmul_mx(
-                            out=h[:, j, :],
-                            lhsT=w_in_codes[:, j * P : (j + 1) * P].bitcast(FP8X4),
-                            lhsT_scale=w_in_scales[:, j * P : (j + 1) * P],
-                            rhs=x_codes[:, m, cols].bitcast(FP8X4),
-                            rhs_scale=x_scales[:, m, cols],
-                            start=True,
-                            stop=True,
-                        )
-                    nc.vector.tensor_tensor(
-                        out=g_grouped[:, m].rearrange("p t (a b) -> p t a b", b=2),
-                        in0=h[:].rearrange("p (a b) t -> p t a b", b=2),
-                        in1=factor[:, :, (i * P) % CHUNK : (i * P) % CHUNK + P, :].rearrange(
-                            "p a t b -> p t a b"
-                        ),
-                        op=ALU.mult,
-                    )
-                    if m > 0:
-                        quantise_g(m - 1, g_grouped, g_codes, g_scales)
-                quantise_g(M2 - 1, g_grouped, g_codes, g_scales)
-                return g_codes, g_scales
+        def take_factor(i):
+            cols = slice(i * P, (i + 1) * P)
+            factors[i] = gate_pool.tile([P, 2, P, 2], F32, name="factor")
+            for a in range(2):
+                pair = slice(2 * a, 2 * a + 2)
+                nc.vector.scalar_tensor_tensor(
+                    out=factors[i][:, a],
+                    in0=rnorm[:, pair, cols].rearrange("p b t -> p t b"),
+                    scalar=1.0 / EPS,
+                    in1=gelus[i][:, pair, :].rearrange("p b t -> p t b"),
+                    op0=ALU.min,
+                    op1=ALU.mult,
+                )
 
-            def project(i, g_codes, g_scales):
-                result = result_pool.tile([P, D, M2], F32)
-                for b in range(BLOCKS):
-                    kept = min(KEEP, D - b * KEEP)
-                    y = y_pool.tile([P, (M2 - 1) * KEEP + WINDOW], F32)
-                    for m in range(M2):
-                        nc.tensor.matmul_mx(
-                            out=y[:, m * KEEP : m * KEEP + WINDOW],
-                            lhsT=g_codes[:, m, :].bitcast(FP8X4),
-                            lhsT_scale=g_scales[:, m, :],
-                            rhs=w_out_codes[:, b, :].bitcast(FP8X4),
-                            rhs_scale=w_out_scales[:, b, :],
-                            start=True,
-                            stop=True,
-                        )
-                    nc.scalar.copy(
-                        out=result[:, b * KEEP : b * KEEP + kept, :],
-                        in_=y[:, 0 : M2 * KEEP].rearrange("p (m d) -> p d m", m=M2)[:, 0:kept, :],
-                    )
-                    if b % 3 == 2:
-                        done = slice((b - 2) * KEEP, b * KEEP + kept)
-                        nc.sync.dma_start(
-                            out=out_rows[i * P : (i + 1) * P, :].rearrange("t (d m) -> t d m", m=M2)[
-                                :, done, :
-                            ],
-                            in_=result[:, done, :],
-                        )
+        def hidden(i, m):
+            if m == 0:
+                g_of[i] = (
+                    g_pool.tile([P, M2, P, PACK], BF16, align_bytes=64, name="g_grouped"),
+                    g_pool.tile([P, M2, P], U32, align_bytes=64, name="g_codes"),
+                    g_pool.tile([P, M2, P], U8, align_bytes=64, name="g_scales"),
+                )
+            h = wide_pool.tile([P, PACK, P], F32, name="wide")
+            for j in range(PACK):
+                nc.tensor.matmul_mx(
+                    out=h[:, j, :],
+                    lhsT=w_in_codes[:, j * P : (j + 1) * P].bitcast(FP8X4),
+                    lhsT_scale=w_in_scales[:, j * P : (j + 1) * P],
+                    rhs=x_codes[:, i, m, :].bitcast(FP8X4),
+                    rhs_scale=x_scales[:, i, m, :],
+                    start=True,
+                    stop=True,
+                )
+            h_of[i, m] = h
 
-            factors = {0: gate(0), 1: gate(1)}
-            g_of = {}
-            for i in range(TILES + 1):
-                if i < TILES:
-                    c = i * P // CHUNK
-                    g_of[i] = hidden(i, factors[c])
-                    if (i + 1) * P % CHUNK == 0 and c + 2 < CHUNKS:
-                        factors[c + 2] = gate(c + 2)
-                if i >= 1:
-                    project(i - 1, g_of[i - 1][0], g_of[i - 1][1])
+        def scale_h(i, m):
+            nc.vector.tensor_tensor(
+                out=g_of[i][0][:, m].rearrange("p t (a b) -> p t a b", b=2),
+                in0=h_of[i, m][:].rearrange("p (a b) t -> p t a b", b=2),
+                in1=factors[i][:].rearrange("p a t b -> p t a b"),
+                op=ALU.mult,
+            )
+
+        def quantise_g(i, m):
+            g_grouped, g_codes, g_scales = g_of[i]
+            nc.vector.quantize_mx(
+                out=g_codes[:, m, :].bitcast(FP8X4),
+                scales=g_scales[:, m, :],
+                in_=g_grouped[:, m].rearrange("p t j -> p (t j)"),
+            )
+
+        results = {}
+
+        def project(i, b):
+            if b == 0:
+                results[i] = result_pool.tile([P, D, M2], F32, name="result")
+            result = results[i]
+            g_codes, g_scales = g_of[i][1:]
+            kept = min(KEEP, D - b * KEEP)
+            if b % 2:
+                y = odd_pool.tile([P, (M2 - 1) * KEEP + WINDOW], F32, name="odd")
+            else:
+                y = even_pool.tile([P, (M2 - 1) * KEEP + WINDOW], F32, name="even")
+            for m in range(M2):
+                nc.tensor.matmul_mx(
+                    out=y[:, m * KEEP : m * KEEP + WINDOW],
+                    lhsT=g_codes[:, m, :].bitcast(FP8X4),
+                    lhsT_scale=g_scales[:, m, :],
+                    rhs=w_out_codes[:, b, :].bitcast(FP8X4),
+                    rhs_scale=w_out_scales[:, b, :],
+                    start=True,
+                    stop=True,
+                )
+            nc.scalar.copy(
+                out=result[:, b * KEEP : b * KEEP + kept, :],
+                in_=y[:, 0 : M2 * KEEP].rearrange("p (m d) -> p d m", m=M2)[:, 0:kept, :],
+            )
+            if b % 3 == 2:
+                done = slice((b - 2) * KEEP, b * KEEP + kept)
+                nc.sync.dma_start(
+                    out=out_rows[i * P : (i + 1) * P, :].rearrange("t (d m) -> t d m", m=M2)[
+                        :, done, :
+                    ],
+                    in_=result[:, done, :],
+                )
+
+        def p2_step(i):
+            order = (("h", 0), ("h", 1), ("y", 0), ("h", 2), ("y", 1), ("h", 3), ("y", 2), ("y", 3), ("h", 4), ("y", 4), ("y", 5))
+            for stage, n in order:
+                if stage == "h" and i < TILES:
+                    hidden(i, n)
+                if stage == "y" and i >= 1:
+                    project(i - 1, n)
+                if stage == "y" and n == 1 and i + 1 < TILES:
+                    take_gelu(i + 1)
+            if i < TILES:
+                for n in range(M2):
+                    scale_h(i, n)
+                    if n > 0:
+                        quantise_g(i, n - 1)
+                    if n == 4 and i + 1 < TILES:
+                        take_factor(i + 1)
+                quantise_g(i, M2 - 1)
+
+        for h in range(TILES, TILES + 3):
+            p1_step(h)
+        take_gelu(0)
+        take_factor(0)
+        for i in range(TILES + 1):
+            p2_step(i)

@@ -44,6 +44,9 @@ def tile_feedforwardse3_pb_t_kernel(tc, x, w_in, scale, bias, w_out, out):
 
         ident = resident.tile([P, P], F32)
         make_identity(nc, ident[:])
+        warm = resident.tile([P, 2], F32)
+        nc.vector.memset(warm[:], 1.0)
+        nc.scalar.activation(out=warm[:, 1:2], in_=warm[:, 0:1], func=ACT.Abs_reciprocal_sqrt)
 
         w_in_codes = resident.tile([P, F], U32, align_bytes=64)
         w_in_scales = resident.tile([P, F], U8, align_bytes=64)
@@ -115,11 +118,135 @@ def tile_feedforwardse3_pb_t_kernel(tc, x, w_in, scale, bias, w_out, out):
         ADDS = lambda i: 0
         planes = {0: (0, 1, 2, 3, 4), 1: (1, 2, 3, 4), 2: (1, 3, 4), 4: (4,)}
 
+        pools = []
+        gelus = {}
+        factors = {}
+        g_of = {}
+        h_of = {}
+
+        def take_gelu(i):
+            cols = slice(i * P, (i + 1) * P)
+            gelus[i] = gate_pool.tile([P, PACK, P], F32, name="gelu")
+            for j in range(PACK):
+                nc.scalar.activation(
+                    out=gelus[i][:, j, :],
+                    in_=norm[:, j, cols],
+                    func=ACT.Gelu,
+                    scale=scale_f32[:, j : j + 1],
+                    bias=bias_f32[:, j : j + 1],
+                )
+
+        def take_factor(i):
+            cols = slice(i * P, (i + 1) * P)
+            factors[i] = gate_pool.tile([P, 2, P, 2], F32, name="factor")
+            for a in range(2):
+                pair = slice(2 * a, 2 * a + 2)
+                nc.vector.scalar_tensor_tensor(
+                    out=factors[i][:, a],
+                    in0=rnorm[:, pair, cols].rearrange("p b t -> p t b"),
+                    scalar=1.0 / EPS,
+                    in1=gelus[i][:, pair, :].rearrange("p b t -> p t b"),
+                    op0=ALU.min,
+                    op1=ALU.mult,
+                )
+
+        def hidden(i, m):
+            if m == 0:
+                g_of[i] = (
+                    pools[0].tile([P, M2, P, PACK], BF16, align_bytes=64, name="g_grouped"),
+                    pools[0].tile([P, M2, P], U32, align_bytes=64, name="g_codes"),
+                    pools[0].tile([P, M2, P], U8, align_bytes=64, name="g_scales"),
+                )
+            h = wide_pool.tile([P, PACK, P], F32, name="wide")
+            for j in range(PACK):
+                nc.tensor.matmul_mx(
+                    out=h[:, j, :],
+                    lhsT=w_in_codes[:, j * P : (j + 1) * P].bitcast(FP8X4),
+                    lhsT_scale=w_in_scales[:, j * P : (j + 1) * P],
+                    rhs=x_codes[:, i, m, :].bitcast(FP8X4),
+                    rhs_scale=x_scales[:, i, m, :],
+                    start=True,
+                    stop=True,
+                )
+            h_of[i, m] = h
+
+        def scale_h(i, m):
+            nc.vector.tensor_tensor(
+                out=g_of[i][0][:, m].rearrange("p t (a b) -> p t a b", b=2),
+                in0=h_of[i, m][:].rearrange("p (a b) t -> p t a b", b=2),
+                in1=factors[i][:].rearrange("p a t b -> p t a b"),
+                op=ALU.mult,
+            )
+
+        def quantise_g(i, m):
+            g_grouped, g_codes, g_scales = g_of[i]
+            nc.vector.quantize_mx(
+                out=g_codes[:, m, :].bitcast(FP8X4),
+                scales=g_scales[:, m, :],
+                in_=g_grouped[:, m].rearrange("p t j -> p (t j)"),
+            )
+
+        results = {}
+
+        def project(i, b):
+            if b == 0:
+                results[i] = pools[1].tile([P, D, M2], F32, name="result")
+            result = results[i]
+            g_codes, g_scales = g_of[i][1:]
+            kept = min(KEEP, D - b * KEEP)
+            if b % 2:
+                y = odd_pool.tile([P, (M2 - 1) * KEEP + WINDOW], F32, name="odd")
+            else:
+                y = even_pool.tile([P, (M2 - 1) * KEEP + WINDOW], F32, name="even")
+            for m in range(M2):
+                nc.tensor.matmul_mx(
+                    out=y[:, m * KEEP : m * KEEP + WINDOW],
+                    lhsT=g_codes[:, m, :].bitcast(FP8X4),
+                    lhsT_scale=g_scales[:, m, :],
+                    rhs=w_out_codes[:, b, :].bitcast(FP8X4),
+                    rhs_scale=w_out_scales[:, b, :],
+                    start=True,
+                    stop=True,
+                )
+            nc.scalar.copy(
+                out=result[:, b * KEEP : b * KEEP + kept, :],
+                in_=y[:, 0 : M2 * KEEP].rearrange("p (m d) -> p d m", m=M2)[:, 0:kept, :],
+            )
+            if b % 3 == 2:
+                done = slice((b - 2) * KEEP, b * KEEP + kept)
+                nc.sync.dma_start(
+                    out=out_rows[i * P : (i + 1) * P, :].rearrange("t (d m) -> t d m", m=M2)[
+                        :, done, :
+                    ],
+                    in_=result[:, done, :],
+                )
+
+        def p2_step(i, order=(("h", 0), ("h", 1), ("y", 0), ("h", 2), ("y", 1), ("h", 3), ("y", 2), ("y", 3), ("h", 4), ("y", 4), ("y", 5)), v_extra={}):
+            for stage, n in order:
+                if stage == "f":
+                    n()
+                if stage == "h" and i < TILES:
+                    hidden(i, n)
+                if stage == "y" and i >= 1:
+                    project(i - 1, n)
+                if stage == "y" and n == 1 and i + 1 < TILES and i >= 2:
+                    take_gelu(i + 1)
+            if i < TILES:
+                for n in range(M2):
+                    scale_h(i, n)
+                    if n > 0:
+                        quantise_g(i, n - 1)
+                    if n == 4 and i + 1 < TILES:
+                        take_factor(i + 1)
+                    if n in v_extra:
+                        v_extra[n]()
+                quantise_g(i, M2 - 1)
+
         def p1_step(h, front=lambda n: None):
             i, k = h - 1, h - 3
             adds = 0 <= i < TILES and ADDS(i) or 0
             front(0)
-            for st in ("sa", 1, "ma", "sb", "r", 2, "n", "mb", 3):
+            for st in ("sa", 1, "ma", "sb", "r", "g", 2, "n", "mb", 3):
                 if isinstance(st, int):
                     front(st)
                 elif st == "sa" and 0 <= k < TILES:
@@ -128,6 +255,9 @@ def tile_feedforwardse3_pb_t_kernel(tc, x, w_in, scale, bias, w_out, out):
                     sum_squares(k, (2, 3), planes[ADDS(k)])
                 elif st == "r" and 0 <= k < TILES:
                     take_root(k)
+                elif st == "g" and k == TILES - 3:
+                    take_gelu(0)
+                    take_gelu(1)
                 elif st == "n" and 0 <= k < TILES:
                     take_norm(k)
                 elif st == "ma" and 0 <= i < TILES:
@@ -211,13 +341,9 @@ def tile_feedforwardse3_pb_t_kernel(tc, x, w_in, scale, bias, w_out, out):
 
             def w_out_group(b, w_out_raw):
                 width = min(WINDOW, D - b * KEEP)
-                nc.gpsimd.tensor_scalar(
+                nc.vector.tensor_copy(
                     out=w_out_grouped[:, b, 0:width, :],
-                    in0=w_out_raw[:, :, b * KEEP : b * KEEP + width].rearrange("p j d -> p d j"),
-                    scalar1=1.0,
-                    scalar2=0.0,
-                    op0=ALU.mult,
-                    op1=ALU.add,
+                    in_=w_out_raw[:, :, b * KEEP : b * KEEP + width].rearrange("p j d -> p d j"),
                 )
 
             def w_out_quantise(b):
@@ -261,10 +387,10 @@ def tile_feedforwardse3_pb_t_kernel(tc, x, w_in, scale, bias, w_out, out):
                     if n == 3:
                         if h + 1 < TILES:
                             split_part(h + 1, slice(3, M2))
-                        if 4 <= h < 4 + BLOCKS:
-                            w_out_group(h - 4, w_out_raw)
-                        if 5 <= h < 5 + BLOCKS:
-                            w_out_quantise(h - 5)
+                        if 7 <= h < 7 + BLOCKS:
+                            w_out_group(h - 7, w_out_raw)
+                        if 8 <= h < 8 + BLOCKS:
+                            w_out_quantise(h - 8)
                         quantise_x(h, B)
                         quantise_x(h, C)
 
@@ -272,129 +398,18 @@ def tile_feedforwardse3_pb_t_kernel(tc, x, w_in, scale, bias, w_out, out):
 
         g_pool = ctx.enter_context(tc.tile_pool(name="g", bufs=2))
         result_pool = ctx.enter_context(tc.tile_pool(name="result", bufs=3))
-        gelus = {}
-        factors = {}
-        g_of = {}
-        h_of = {}
-
-        def take_gelu(i):
-            cols = slice(i * P, (i + 1) * P)
-            gelus[i] = gate_pool.tile([P, PACK, P], F32, name="gelu")
-            for j in range(PACK):
-                nc.scalar.activation(
-                    out=gelus[i][:, j, :],
-                    in_=norm[:, j, cols],
-                    func=ACT.Gelu,
-                    scale=scale_f32[:, j : j + 1],
-                    bias=bias_f32[:, j : j + 1],
-                )
-
-        def take_factor(i):
-            cols = slice(i * P, (i + 1) * P)
-            factors[i] = gate_pool.tile([P, 2, P, 2], F32, name="factor")
-            for a in range(2):
-                pair = slice(2 * a, 2 * a + 2)
-                nc.vector.scalar_tensor_tensor(
-                    out=factors[i][:, a],
-                    in0=rnorm[:, pair, cols].rearrange("p b t -> p t b"),
-                    scalar=1.0 / EPS,
-                    in1=gelus[i][:, pair, :].rearrange("p b t -> p t b"),
-                    op0=ALU.min,
-                    op1=ALU.mult,
-                )
-
-        def hidden(i, m):
-            if m == 0:
-                g_of[i] = (
-                    g_pool.tile([P, M2, P, PACK], BF16, align_bytes=64, name="g_grouped"),
-                    g_pool.tile([P, M2, P], U32, align_bytes=64, name="g_codes"),
-                    g_pool.tile([P, M2, P], U8, align_bytes=64, name="g_scales"),
-                )
-            h = wide_pool.tile([P, PACK, P], F32, name="wide")
-            for j in range(PACK):
-                nc.tensor.matmul_mx(
-                    out=h[:, j, :],
-                    lhsT=w_in_codes[:, j * P : (j + 1) * P].bitcast(FP8X4),
-                    lhsT_scale=w_in_scales[:, j * P : (j + 1) * P],
-                    rhs=x_codes[:, i, m, :].bitcast(FP8X4),
-                    rhs_scale=x_scales[:, i, m, :],
-                    start=True,
-                    stop=True,
-                )
-            h_of[i, m] = h
-
-        def scale_h(i, m):
-            nc.vector.tensor_tensor(
-                out=g_of[i][0][:, m].rearrange("p t (a b) -> p t a b", b=2),
-                in0=h_of[i, m][:].rearrange("p (a b) t -> p t a b", b=2),
-                in1=factors[i][:].rearrange("p a t b -> p t a b"),
-                op=ALU.mult,
-            )
-
-        def quantise_g(i, m):
-            g_grouped, g_codes, g_scales = g_of[i]
-            nc.vector.quantize_mx(
-                out=g_codes[:, m, :].bitcast(FP8X4),
-                scales=g_scales[:, m, :],
-                in_=g_grouped[:, m].rearrange("p t j -> p (t j)"),
-            )
-
-        results = {}
-
-        def project(i, b):
-            if b == 0:
-                results[i] = result_pool.tile([P, D, M2], F32, name="result")
-            result = results[i]
-            g_codes, g_scales = g_of[i][1:]
-            kept = min(KEEP, D - b * KEEP)
-            if b % 2:
-                y = odd_pool.tile([P, (M2 - 1) * KEEP + WINDOW], F32, name="odd")
-            else:
-                y = even_pool.tile([P, (M2 - 1) * KEEP + WINDOW], F32, name="even")
-            for m in range(M2):
-                nc.tensor.matmul_mx(
-                    out=y[:, m * KEEP : m * KEEP + WINDOW],
-                    lhsT=g_codes[:, m, :].bitcast(FP8X4),
-                    lhsT_scale=g_scales[:, m, :],
-                    rhs=w_out_codes[:, b, :].bitcast(FP8X4),
-                    rhs_scale=w_out_scales[:, b, :],
-                    start=True,
-                    stop=True,
-                )
-            nc.scalar.copy(
-                out=result[:, b * KEEP : b * KEEP + kept, :],
-                in_=y[:, 0 : M2 * KEEP].rearrange("p (m d) -> p d m", m=M2)[:, 0:kept, :],
-            )
-            if b % 3 == 2:
-                done = slice((b - 2) * KEEP, b * KEEP + kept)
-                nc.sync.dma_start(
-                    out=out_rows[i * P : (i + 1) * P, :].rearrange("t (d m) -> t d m", m=M2)[
-                        :, done, :
-                    ],
-                    in_=result[:, done, :],
-                )
-
-        def p2_step(i):
-            order = (("h", 0), ("h", 1), ("y", 0), ("h", 2), ("y", 1), ("h", 3), ("y", 2), ("y", 3), ("h", 4), ("y", 4), ("y", 5))
-            for stage, n in order:
-                if stage == "h" and i < TILES:
-                    hidden(i, n)
-                if stage == "y" and i >= 1:
-                    project(i - 1, n)
-                if stage == "y" and n == 1 and i + 1 < TILES:
-                    take_gelu(i + 1)
-            if i < TILES:
-                for n in range(M2):
-                    scale_h(i, n)
-                    if n > 0:
-                        quantise_g(i, n - 1)
-                    if n == 4 and i + 1 < TILES:
-                        take_factor(i + 1)
-                quantise_g(i, M2 - 1)
-
-        for h in range(TILES, TILES + 3):
-            p1_step(h)
-        take_gelu(0)
+        pools.extend((g_pool, result_pool))
+        p1_step(TILES)
         take_factor(0)
-        for i in range(TILES + 1):
+        sum_squares(14, (0, 1, 2, 3), planes[ADDS(14)])
+        take_root(14)
+
+        def last_sum():
+            sum_squares(15, (0, 1, 2, 3), planes[ADDS(15)])
+            take_root(15)
+            take_gelu(2)
+
+        p2_step(0, order=(("h", 0), ("h", 1), ("h", 2), ("h", 3), ("h", 4), ("f", last_sum)), v_extra={4: lambda: take_norm(14)})
+        p2_step(1, v_extra={0: lambda: take_norm(15)})
+        for i in range(2, TILES + 1):
             p2_step(i)

@@ -178,12 +178,12 @@ def tile_feedforwardse3_pb_t_kernel(tc, x, w_in, scale, bias, w_out, out):
                 op=ALU.mult,
             )
 
-        def quantise_g(i, m):
+        def quantise_g(i, ms):
             g_grouped, g_codes, g_scales = g_of[i]
             nc.vector.quantize_mx(
-                out=g_codes[:, m, :].bitcast(FP8X4),
-                scales=g_scales[:, m, :],
-                in_=g_grouped[:, m].rearrange("p t j -> p (t j)"),
+                out=g_codes[:, ms, :].rearrange("p m t -> p (m t)").bitcast(FP8X4),
+                scales=g_scales[:, ms, :].rearrange("p m t -> p (m t)"),
+                in_=g_grouped[:, ms].rearrange("p m t j -> p (m t j)"),
             )
 
         results = {}
@@ -208,12 +208,15 @@ def tile_feedforwardse3_pb_t_kernel(tc, x, w_in, scale, bias, w_out, out):
                     start=True,
                     stop=True,
                 )
-            nc.scalar.copy(
+            copy = nc.vector.tensor_copy if i == TILES - 1 and b % 2 else nc.scalar.copy
+            copy(
                 out=result[:, b * KEEP : b * KEEP + kept, :],
                 in_=y[:, 0 : M2 * KEEP].rearrange("p (m d) -> p d m", m=M2)[:, 0:kept, :],
             )
-            if b % 3 == 2:
-                done = slice((b - 2) * KEEP, b * KEEP + kept)
+            stores = (2, 4, 5) if i == TILES - 1 else (2, 5)
+            if b in stores:
+                first = max((s + 1 for s in stores if s < b), default=0)
+                done = slice(first * KEEP, b * KEEP + kept)
                 nc.sync.dma_start(
                     out=out_rows[i * P : (i + 1) * P, :].rearrange("t (d m) -> t d m", m=M2)[
                         :, done, :
@@ -229,18 +232,17 @@ def tile_feedforwardse3_pb_t_kernel(tc, x, w_in, scale, bias, w_out, out):
                     hidden(i, n)
                 if stage == "y" and i >= 1:
                     project(i - 1, n)
-                if stage == "y" and n == 1 and i + 1 < TILES and i >= 2:
+                if stage == "y" and n == 0 and i + 1 < TILES and i >= 2:
                     take_gelu(i + 1)
             if i < TILES:
                 for n in range(M2):
                     scale_h(i, n)
-                    if n > 0:
-                        quantise_g(i, n - 1)
-                    if n == 4 and i + 1 < TILES:
+                    for a, b in {2: ((0, 2),), 4: ((2, 4), (4, 5))}.get(n, ()):
+                        quantise_g(i, slice(a, b))
+                    if n == 3 and i + 1 < TILES:
                         take_factor(i + 1)
                     if n in v_extra:
                         v_extra[n]()
-                quantise_g(i, M2 - 1)
 
         def p1_step(h, front=lambda n: None):
             i, k = h - 1, h - 3
@@ -287,10 +289,10 @@ def tile_feedforwardse3_pb_t_kernel(tc, x, w_in, scale, bias, w_out, out):
                 loaded[i] = loaded_pool.tile([P, ROW], BF16, name="x_sb")
                 nc.sync.dma_start(out=loaded[i][:], in_=x_rows[i * P : (i + 1) * P, :])
 
-            def split_part(i, ms):
+            def split_part(i, ms, copy=nc.vector.tensor_copy):
                 if ms.start == 0:
                     split[i] = split_pool.tile([P, M2, D], BF16, name="x_split")
-                nc.vector.tensor_copy(
+                copy(
                     out=split[i][:, ms, :].rearrange("p m (c i) -> p c m i", i=PACK),
                     in_=loaded[i][:].rearrange("p (c i m) -> p c m i", i=PACK, m=M2)[:, :, ms, :],
                 )
@@ -331,9 +333,12 @@ def tile_feedforwardse3_pb_t_kernel(tc, x, w_in, scale, bias, w_out, out):
             nc.sync.dma_start(out=bias_raw[:], in_=bias.rearrange("a b (p j) -> (a b p) j", j=PACK))
 
             w_in_grouped = weights.tile([P, PACK, P, PACK], BF16, align_bytes=64)
-            nc.scalar.copy(
-                out=w_in_grouped[:], in_=w_in_raw[:].rearrange("p i (q j) -> p j q i", j=PACK)
-            )
+
+            def w_in_group(js, copy):
+                copy(
+                    out=w_in_grouped[:, js],
+                    in_=w_in_raw[:].rearrange("p i (q j) -> p j q i", j=PACK)[:, js],
+                )
             w_out_grouped = weights.tile([P, BLOCKS, WINDOW, PACK], BF16, align_bytes=64)
             nc.gpsimd.memset(w_out_grouped[:, BLOCKS - 1], 0.0)
             nc.gpsimd.tensor_copy(out=scale_f32[:], in_=scale_raw[:])
@@ -354,8 +359,14 @@ def tile_feedforwardse3_pb_t_kernel(tc, x, w_in, scale, bias, w_out, out):
                 )
 
             A, B, C = (0, 1), (2, 3), (4,)
-            for ms in (slice(0, 3), slice(3, M2)):
-                split_part(0, ms)
+            split_part(0, slice(0, 3))
+            split_part(0, slice(3, M2), nc.scalar.copy)
+            w_in_group(slice(0, 2), nc.vector.tensor_copy)
+            w_in_group(slice(2, PACK), nc.scalar.copy)
+
+            def last_quantise(n):
+                if n == 1:
+                    quantise_x(TILES - 1, C)
 
             for h in range(TILES):
                 if h + 4 < TILES:
@@ -370,36 +381,36 @@ def tile_feedforwardse3_pb_t_kernel(tc, x, w_in, scale, bias, w_out, out):
                     if n == 1:
                         transpose_x(h, A)
                         group_x(h, A, nc.vector.tensor_copy)
+                        if h > 0:
+                            quantise_x(h - 1, C)
                         if h + 1 < TILES:
                             split_part(h + 1, slice(0, 3))
                         quantise_x(h, A)
-                    if n == 2:
-                        transpose_x(h, B)
-                        group_x(h, B, nc.scalar.copy)
-                        transpose_x(h, C)
-                        group_x(h, C, nc.vector.tensor_copy)
                         if h == 0:
                             nc.vector.quantize_mx(
                                 out=w_in_codes[:].bitcast(FP8X4),
                                 scales=w_in_scales[:],
                                 in_=w_in_grouped[:].rearrange("p j q i -> p (j q i)"),
                             )
-                    if n == 3:
                         if h + 1 < TILES:
                             split_part(h + 1, slice(3, M2))
                         if 7 <= h < 7 + BLOCKS:
                             w_out_group(h - 7, w_out_raw)
                         if 8 <= h < 8 + BLOCKS:
                             w_out_quantise(h - 8)
+                    if n == 2:
+                        transpose_x(h, B)
+                        group_x(h, B, nc.scalar.copy)
+                        transpose_x(h, C)
                         quantise_x(h, B)
-                        quantise_x(h, C)
+                        group_x(h, C, nc.vector.tensor_copy)
 
                 p1_step(h, front)
 
+            p1_step(TILES, last_quantise)
         g_pool = ctx.enter_context(tc.tile_pool(name="g", bufs=2))
         result_pool = ctx.enter_context(tc.tile_pool(name="result", bufs=3))
         pools.extend((g_pool, result_pool))
-        p1_step(TILES)
         take_factor(0)
         sum_squares(14, (0, 1, 2, 3), planes[ADDS(14)])
         take_root(14)

@@ -115,8 +115,8 @@ def tile_feedforwardse3_pb_t_kernel(tc, x, w_in, scale, bias, w_out, out):
                 op1=ALU.mult,
             )
 
-        ADDS = lambda i: 0
-        planes = {0: (0, 1, 2, 3, 4), 1: (1, 2, 3, 4), 2: (1, 3, 4), 4: (4,)}
+        ADDS = lambda i: 7 if i % 2 else 0
+        planes = {0: (0, 1, 2, 3, 4), 1: (1, 2, 3, 4), 2: (1, 3, 4), 4: (4,), 3: (0, 1, 3, 4), 5: (0, 1, 2, 4), 7: (1, 2, 3, 4), 8: (1, 3, 4)}
 
         pools = []
         gelus = {}
@@ -247,8 +247,10 @@ def tile_feedforwardse3_pb_t_kernel(tc, x, w_in, scale, bias, w_out, out):
         def p1_step(h, front=lambda n: None):
             i, k = h - 1, h - 3
             adds = 0 <= i < TILES and ADDS(i) or 0
-            front(0)
-            for st in ("sa", 1, "ma", "sb", "r", "g", 2, "n", "mb", 3):
+            order = ("sa", 1, "ma", "sb", "r", "g", 2, "n", "mb", 3)
+            if h == 1:
+                order = ("sa", 1, "ma", "sb", "r", "g", 2, "n", "mb", 3)
+            for st in order:
                 if isinstance(st, int):
                     front(st)
                 elif st == "sa" and 0 <= k < TILES:
@@ -264,12 +266,19 @@ def tile_feedforwardse3_pb_t_kernel(tc, x, w_in, scale, bias, w_out, out):
                     take_norm(k)
                 elif st == "ma" and 0 <= i < TILES:
                     multiply_and_square(i, (0, 1))
-                    if adds > 0:
+                    if adds in (1, 2, 4):
                         add_squares(i, 1, 0, nc.gpsimd if adds < 4 else nc.vector)
                 elif st == "mb" and 0 <= i < TILES:
                     multiply_and_square(i, (2, 3, 4))
-                    if adds == 2:
+                    if adds in (2, 3):
                         add_squares(i, 3, 2, nc.gpsimd)
+                    if adds == 5:
+                        add_squares(i, 4, 3, nc.gpsimd)
+                    if adds == 7:
+                        add_squares(i, 1, 0, nc.vector)
+                    if adds == 8:
+                        add_squares(i, 1, 0, nc.vector)
+                        add_squares(i, 3, 2, nc.vector)
                     if adds == 4:
                         add_squares(i, 2, 1, nc.vector)
                         add_squares(i, 3, 2, nc.vector)
@@ -367,6 +376,10 @@ def tile_feedforwardse3_pb_t_kernel(tc, x, w_in, scale, bias, w_out, out):
             def last_quantise(n):
                 if n == 1:
                     quantise_x(TILES - 1, C)
+                    for b in range(max(0, TILES - 16), BLOCKS):
+                        w_out_group(b, w_out_raw)
+                    for b in range(max(0, TILES - 1 - 16), BLOCKS):
+                        w_out_quantise(b)
 
             for h in range(TILES):
                 if h + 4 < TILES:
@@ -394,10 +407,10 @@ def tile_feedforwardse3_pb_t_kernel(tc, x, w_in, scale, bias, w_out, out):
                             )
                         if h + 1 < TILES:
                             split_part(h + 1, slice(3, M2))
-                        if 7 <= h < 7 + BLOCKS:
-                            w_out_group(h - 7, w_out_raw)
-                        if 8 <= h < 8 + BLOCKS:
-                            w_out_quantise(h - 8)
+                        if 16 <= h < 16 + BLOCKS:
+                            w_out_group(h - 16, w_out_raw)
+                        if 16 + 1 <= h < 16 + 1 + BLOCKS:
+                            w_out_quantise(h - 16 - 1)
                     if n == 2:
                         transpose_x(h, B)
                         group_x(h, B, nc.scalar.copy)

@@ -247,7 +247,7 @@ def tile_feedforwardse3_pb_t_kernel(tc, x, w_in, scale, bias, w_out, out):
         def p1_step(h, front=lambda n: None):
             i, k = h - 1, h - 3
             adds = 0 <= i < TILES and ADDS(i) or 0
-            order = ("sa", 1, "ma", "sb", "r", "g", 2, "n", "mb", 3)
+            order = ("sa", 1, "ma", "sb", "r", "g", 2, "n", "mb", "G", 3)
             if h == 1:
                 order = ("sa", 1, "ma", "sb", "r", "g", 2, "n", "mb", 3)
             for st in order:
@@ -261,6 +261,7 @@ def tile_feedforwardse3_pb_t_kernel(tc, x, w_in, scale, bias, w_out, out):
                     take_root(k)
                 elif st == "g" and k == TILES - 3:
                     take_gelu(0)
+                elif st == "G" and k == TILES - 3:
                     take_gelu(1)
                 elif st == "n" and 0 <= k < TILES:
                     take_norm(k)
@@ -413,7 +414,7 @@ def tile_feedforwardse3_pb_t_kernel(tc, x, w_in, scale, bias, w_out, out):
                             w_out_quantise(h - 16 - 1)
                     if n == 2:
                         transpose_x(h, B)
-                        group_x(h, B, nc.scalar.copy)
+                        group_x(h, B, nc.scalar.copy if h < 15 else nc.vector.tensor_copy)
                         transpose_x(h, C)
                         quantise_x(h, B)
                         group_x(h, C, nc.vector.tensor_copy)

@@ -48,12 +48,12 @@ def tile_feedforwardse3_pb_t_kernel(tc, x, w_in, scale, bias, w_out, out):
         nc.vector.memset(warm[:], 1.0)
         nc.scalar.activation(out=warm[:, 1:2], in_=warm[:, 0:1], func=ACT.Abs_reciprocal_sqrt)
 
-        w_in_codes = resident.tile([P, F], U32, align_bytes=64)
-        w_in_scales = resident.tile([P, F], U8, align_bytes=64)
-        w_out_codes = resident.tile([P, BLOCKS, WINDOW], U32, align_bytes=64)
-        w_out_scales = resident.tile([P, BLOCKS, WINDOW], U8, align_bytes=64)
-        x_codes = resident.tile([P, TILES, M2, P], U32, align_bytes=64)
-        x_scales = resident.tile([P, TILES, M2, P], U8, align_bytes=64)
+        w_in_codes = resident.tile([P, F], U32, align_bytes=256)
+        w_in_scales = resident.tile([P, F], U8, align_bytes=256)
+        w_out_codes = resident.tile([P, BLOCKS, WINDOW], U32, align_bytes=256)
+        w_out_scales = resident.tile([P, BLOCKS, WINDOW], U8, align_bytes=256)
+        x_codes = resident.tile([P, TILES, M2, P], U32, align_bytes=256)
+        x_scales = resident.tile([P, TILES, M2, P], U8, align_bytes=256)
 
         norm = resident.tile([P, PACK, TOKENS], F32)
         rnorm = resident.tile([P, PACK, TOKENS], F32)
@@ -154,8 +154,8 @@ def tile_feedforwardse3_pb_t_kernel(tc, x, w_in, scale, bias, w_out, out):
             if m == 0:
                 g_of[i] = (
                     pools[0].tile([P, M2, P, PACK], BF16, align_bytes=64, name="g_grouped"),
-                    pools[0].tile([P, M2, P], U32, align_bytes=64, name="g_codes"),
-                    pools[0].tile([P, M2, P], U8, align_bytes=64, name="g_scales"),
+                    pools[0].tile([P, M2, P], U32, align_bytes=256, name="g_codes"),
+                    pools[0].tile([P, M2, P], U8, align_bytes=256, name="g_scales"),
                 )
             h = wide_pool.tile([P, PACK, P], F32, name="wide")
             for j in range(PACK):

from contextlib import ExitStack

import concourse.mybir as mybir
from concourse.masks import make_identity

F32 = mybir.dt.float32
BF16 = mybir.dt.bfloat16
U32 = mybir.dt.uint32
U8 = mybir.dt.uint8
FP8X4 = mybir.dt.float8_e4m3fn_x4
ACT = mybir.ActivationFunctionType
ALU = mybir.AluOpType

P = 128
PACK = 4
TOKENS = 4 * 512
D = 512
F = 512
M2 = 5
ROW = D * M2
EPS = 1e-12

TILES = TOKENS // P
WINDOW = 128
KEEP = 96
BLOCKS = -(-D // KEEP)

FLOPS = 2 * 2 * TOKENS * M2 * D * F


def tile_feedforwardse3_pb_t_kernel(tc, x, w_in, scale, bias, w_out, out):
    nc = tc.nc
    x_rows = x.rearrange("b n d m -> (b n) (d m)")
    out_rows = out.rearrange("b n d m -> (b n) (d m)")

    with ExitStack() as ctx:
        ctx.enter_context(tc.manual_schedule())
        resident = ctx.enter_context(tc.tile_pool(name="resident", bufs=1))
        gate_pool = ctx.enter_context(tc.tile_pool(name="gate", bufs=2))
        square_pool = ctx.enter_context(tc.tile_pool(name="squares", bufs=2))
        wide_pool = ctx.enter_context(tc.psum_pool(name="wide", bufs=4))
        even_pool = ctx.enter_context(tc.psum_pool(name="even", bufs=2))
        odd_pool = ctx.enter_context(tc.psum_pool(name="odd", bufs=2))

        ident = resident.tile([P, P], F32)
        make_identity(nc, ident[:])
        warm = resident.tile([P, 2], F32)
        nc.vector.memset(warm[:], 1.0)
        nc.scalar.activation(out=warm[:, 1:2], in_=warm[:, 0:1], func=ACT.Abs_reciprocal_sqrt)

        w_in_codes = resident.tile([P, F], U32, align_bytes=256)
        w_in_scales = resident.tile([P, F], U8, align_bytes=256)
        w_out_codes = resident.tile([P, BLOCKS, WINDOW], U32, align_bytes=256)
        w_out_scales = resident.tile([P, BLOCKS, WINDOW], U8, align_bytes=256)
        x_codes = resident.tile([P, TILES, M2, P], U32, align_bytes=256)
        x_scales = resident.tile([P, TILES, M2, P], U8, align_bytes=256)

        norm = resident.tile([P, PACK, TOKENS], F32)
        rnorm = resident.tile([P, PACK, TOKENS], F32)
        scale_f32 = resident.tile([P, PACK], F32)
        bias_f32 = resident.tile([P, PACK], F32)

        squares = {}
        sums = {}

        def multiply_and_square(i, ms):
            for m in ms:
                ht = wide_pool.tile([P, F], F32, name="wide")
                nc.tensor.matmul_mx(
                    out=ht[:],
                    lhsT=x_codes[:, i, m, :].bitcast(FP8X4),
                    lhsT_scale=x_scales[:, i, m, :],
                    rhs=w_in_codes[:].bitcast(FP8X4),
                    rhs_scale=w_in_scales[:],
                    start=True,
                    stop=True,
                )
                sq = square_pool.tile([P, F], F32, name="sq%d" % m)
                nc.scalar.activation(out=sq[:], in_=ht[:], func=ACT.Square)
                squares[i, m] = sq

        def add_squares(i, m, n, eng):
            eng.tensor_tensor(
                out=squares[i, m][:], in0=squares[i, m][:], in1=squares[i, n][:], op=ALU.add
            )

        def sum_squares(i, js, planes):
            if js[0] == 0:
                sums[i] = odd_pool.tile([P, PACK, P], F32, name="odd")
            for j in js:
                for n, m in enumerate(planes):
                    nc.tensor.matmul(
                        out=sums[i][:, j, :],
                        lhsT=squares[i, m][:, j * P : (j + 1) * P],
                        rhs=ident[:],
                        is_transpose=True,
                        start=(n == 0),
                        stop=(n == len(planes) - 1),
                    )

        def take_root(i):
            cols = slice(i * P, (i + 1) * P)
            nc.scalar.activation(
                out=rnorm[:, :, cols], in_=sums[i][:], func=ACT.Abs_reciprocal_sqrt
            )

        def take_norm(i):
            cols = slice(i * P, (i + 1) * P)
            nc.vector.scalar_tensor_tensor(
                out=norm[:, :, cols],
                in0=rnorm[:, :, cols],
                scalar=1.0 / EPS,
                in1=sums[i][:],
                op0=ALU.min,
                op1=ALU.mult,
            )

        ADDS = lambda i: 7 if i % 2 else 0
        planes = {0: (0, 1, 2, 3, 4), 1: (1, 2, 3, 4), 2: (1, 3, 4), 4: (4,), 3: (0, 1, 3, 4), 5: (0, 1, 2, 4), 7: (1, 2, 3, 4), 8: (1, 3, 4)}

        pools = []
        gelus = {}
        factors = {}
        g_of = {}
        h_of = {}

        def take_gelu(i):
            cols = slice(i * P, (i + 1) * P)
            gelus[i] = gate_pool.tile([P, PACK, P], F32, name="gelu")
            for j in range(PACK):
                nc.scalar.activation(
                    out=gelus[i][:, j, :],
                    in_=norm[:, j, cols],
                    func=ACT.Gelu,
                    scale=scale_f32[:, j : j + 1],
                    bias=bias_f32[:, j : j + 1],
                )

        def take_factor(i):
            cols = slice(i * P, (i + 1) * P)
            factors[i] = gate_pool.tile([P, 2, P, 2], F32, name="factor")
            for a in range(2):
                pair = slice(2 * a, 2 * a + 2)
                nc.vector.scalar_tensor_tensor(
                    out=factors[i][:, a],
                    in0=rnorm[:, pair, cols].rearrange("p b t -> p t b"),
                    scalar=1.0 / EPS,
                    in1=gelus[i][:, pair, :].rearrange("p b t -> p t b"),
                    op0=ALU.min,
                    op1=ALU.mult,
                )

        def hidden(i, m):
            if m == 0:
                g_of[i] = (
                    pools[0].tile([P, M2, P, PACK], BF16, align_bytes=64, name="g_grouped"),
                    pools[0].tile([P, M2, P], U32, align_bytes=256, name="g_codes"),
                    pools[0].tile([P, M2, P], U8, align_bytes=256, name="g_scales"),
                )
            h = wide_pool.tile([P, PACK, P], F32, name="wide")
            for j in range(PACK):
                nc.tensor.matmul_mx(
                    out=h[:, j, :],
                    lhsT=w_in_codes[:, j * P : (j + 1) * P].bitcast(FP8X4),
                    lhsT_scale=w_in_scales[:, j * P : (j + 1) * P],
                    rhs=x_codes[:, i, m, :].bitcast(FP8X4),
                    rhs_scale=x_scales[:, i, m, :],
                    start=True,
                    stop=True,
                )
            h_of[i, m] = h

        def scale_h(i, m):
            nc.vector.tensor_tensor(
                out=g_of[i][0][:, m].rearrange("p t (a b) -> p t a b", b=2),
                in0=h_of[i, m][:].rearrange("p (a b) t -> p t a b", b=2),
                in1=factors[i][:].rearrange("p a t b -> p t a b"),
                op=ALU.mult,
            )

        def quantise_g(i, ms):
            g_grouped, g_codes, g_scales = g_of[i]
            nc.vector.quantize_mx(
                out=g_codes[:, ms, :].rearrange("p m t -> p (m t)").bitcast(FP8X4),
                scales=g_scales[:, ms, :].rearrange("p m t -> p (m t)"),
                in_=g_grouped[:, ms].rearrange("p m t j -> p (m t j)"),
            )

        results = {}

        def project(i, b):
            if b == 0:
                results[i] = pools[1].tile([P, D, M2], F32, name="result")
            result = results[i]
            g_codes, g_scales = g_of[i][1:]
            kept = min(KEEP, D - b * KEEP)
            if b % 2:
                y = odd_pool.tile([P, (M2 - 1) * KEEP + WINDOW], F32, name="odd")
            else:
                y = even_pool.tile([P, (M2 - 1) * KEEP + WINDOW], F32, name="even")
            for m in range(M2):
                nc.tensor.matmul_mx(
                    out=y[:, m * KEEP : m * KEEP + WINDOW],
                    lhsT=g_codes[:, m, :].bitcast(FP8X4),
                    lhsT_scale=g_scales[:, m, :],
                    rhs=w_out_codes[:, b, :].bitcast(FP8X4),
                    rhs_scale=w_out_scales[:, b, :],
                    start=True,
                    stop=True,
                )
            copy = nc.vector.tensor_copy if i == TILES - 1 and b % 2 else nc.scalar.copy
            copy(
                out=result[:, b * KEEP : b * KEEP + kept, :],
                in_=y[:, 0 : M2 * KEEP].rearrange("p (m d) -> p d m", m=M2)[:, 0:kept, :],
            )
            stores = (2, 4, 5) if i == TILES - 1 else (2, 5)
            if b in stores:
                first = max((s + 1 for s in stores if s < b), default=0)
                done = slice(first * KEEP, b * KEEP + kept)
                nc.sync.dma_start(
                    out=out_rows[i * P : (i + 1) * P, :].rearrange("t (d m) -> t d m", m=M2)[
                        :, done, :
                    ],
                    in_=result[:, done, :],
                )

        def p2_step(i, order=(("h", 0), ("h", 1), ("y", 0), ("h", 2), ("y", 1), ("h", 3), ("y", 2), ("y", 3), ("h", 4), ("y", 4), ("y", 5)), v_extra={}):
            for stage, n in order:
                if stage == "f":
                    n()
                if stage == "h" and i < TILES:
                    hidden(i, n)
                if stage == "y" and i >= 1:
                    project(i - 1, n)
                if stage == "y" and n == 0 and i + 1 < TILES and i >= 2:
                    take_gelu(i + 1)
            if i < TILES:
                for n in range(M2):
                    scale_h(i, n)
                    for a, b in {2: ((0, 2),), 4: ((2, 4), (4, 5))}.get(n, ()):
                        quantise_g(i, slice(a, b))
                    if n == 3 and i + 1 < TILES:
                        take_factor(i + 1)
                    if n in v_extra:
                        v_extra[n]()

        def p1_step(h, front=lambda n: None):
            i, k = h - 1, h - 3
            adds = 0 <= i < TILES and ADDS(i) or 0
            order = ("sa", 1, "ma", "sb", "r", "g", 2, "n", "mb", "G", 3)
            if h == 1:
                order = ("sa", 1, "ma", "sb", "r", "g", 2, "n", "mb", 3)
            for st in order:
                if isinstance(st, int):
                    front(st)
                elif st == "sa" and 0 <= k < TILES:
                    sum_squares(k, (0, 1), planes[ADDS(k)])
                elif st == "sb" and 0 <= k < TILES:
                    sum_squares(k, (2, 3), planes[ADDS(k)])
                elif st == "r" and 0 <= k < TILES:
                    take_root(k)
                elif st == "g" and k == TILES - 3:
                    take_gelu(0)
                elif st == "G" and k == TILES - 3:
                    take_gelu(1)
                elif st == "n" and 0 <= k < TILES:
                    take_norm(k)
                elif st == "ma" and 0 <= i < TILES:
                    multiply_and_square(i, (0, 1))
                    if adds in (1, 2, 4):
                        add_squares(i, 1, 0, nc.gpsimd if adds < 4 else nc.vector)
                elif st == "mb" and 0 <= i < TILES:
                    multiply_and_square(i, (2, 3, 4))
                    if adds in (2, 3):
                        add_squares(i, 3, 2, nc.gpsimd)
                    if adds == 5:
                        add_squares(i, 4, 3, nc.gpsimd)
                    if adds == 7:
                        add_squares(i, 1, 0, nc.vector)
                    if adds == 8:
                        add_squares(i, 1, 0, nc.vector)
                        add_squares(i, 3, 2, nc.vector)
                    if adds == 4:
                        add_squares(i, 2, 1, nc.vector)
                        add_squares(i, 3, 2, nc.vector)
                        add_squares(i, 4, 3, nc.vector)

        with tc.tile_pool(name="weights", bufs=1) as weights, tc.tile_pool(
            name="loaded", bufs=4
        ) as loaded_pool, tc.tile_pool(name="split", bufs=2) as split_pool, tc.tile_pool(
            name="grouped", bufs=4
        ) as grouped_pool:
            loaded = {}
            split = {}
            xt = {}
            grouped = {}

            def load_tile(i):
                loaded[i] = loaded_pool.tile([P, ROW], BF16, name="x_sb")
                nc.sync.dma_start(out=loaded[i][:], in_=x_rows[i * P : (i + 1) * P, :])

            def split_part(i, ms, copy=nc.vector.tensor_copy):
                if ms.start == 0:
                    split[i] = split_pool.tile([P, M2, D], BF16, name="x_split")
                copy(
                    out=split[i][:, ms, :].rearrange("p m (c i) -> p c m i", i=PACK),
                    in_=loaded[i][:].rearrange("p (c i m) -> p c m i", i=PACK, m=M2)[:, :, ms, :],
                )

            def transpose_x(i, ms):
                words = split[i][:].bitcast(F32).rearrange("p m (u q) -> p m u q", u=2)
                xt[i, ms] = even_pool.tile([P, len(ms), 2, P], F32, name="even")
                for n, m in enumerate(ms):
                    for u in range(2):
                        nc.tensor.transpose(xt[i, ms][:, n, u, :], words[:, m, u, :], ident[:])

            def group_x(i, ms, copy):
                grouped[i, ms] = grouped_pool.tile([P, len(ms), P, PACK], BF16, align_bytes=64, name="grouped%d" % len(ms))
                copy(
                    out=grouped[i, ms][:].rearrange("p m t i -> p m (t i)").bitcast(F32).rearrange("p m (t u) -> p m t u", u=2),
                    in_=xt[i, ms][:].rearrange("p m u t -> p m t u"),
                )

            def quantise_x(i, ms):
                nc.vector.quantize_mx(
                    out=x_codes[:, i, ms[0] : ms[-1] + 1, :].rearrange("p m t -> p (m t)").bitcast(FP8X4),
                    scales=x_scales[:, i, ms[0] : ms[-1] + 1, :].rearrange("p m t -> p (m t)"),
                    in_=grouped[i, ms][:].rearrange("p m t i -> p (m t i)"),
                )

            load_tile(0)
            w_in_raw = weights.tile([P, PACK, F], BF16)
            nc.sync.dma_start(
                out=w_in_raw[:].rearrange("p (u e) f -> p u e f", u=2),
                in_=w_in.rearrange("(u p e) f -> p u e f", u=2, e=2),
            )
            load_tile(1)
            load_tile(2)
            load_tile(3)
            scale_raw = weights.tile([P, PACK], BF16)
            nc.sync.dma_start(out=scale_raw[:], in_=scale.rearrange("a b (p j) -> (a b p) j", j=PACK))
            bias_raw = weights.tile([P, PACK], BF16)
            nc.sync.dma_start(out=bias_raw[:], in_=bias.rearrange("a b (p j) -> (a b p) j", j=PACK))

            w_in_grouped = weights.tile([P, PACK, P, PACK], BF16, align_bytes=64)

            def w_in_group(js, copy):
                copy(
                    out=w_in_grouped[:, js],
                    in_=w_in_raw[:].rearrange("p i (q j) -> p j q i", j=PACK)[:, js],
                )
            w_out_grouped = weights.tile([P, BLOCKS, WINDOW, PACK], BF16, align_bytes=64)
            nc.gpsimd.memset(w_out_grouped[:, BLOCKS - 1], 0.0)
            nc.gpsimd.tensor_copy(out=scale_f32[:], in_=scale_raw[:])
            nc.gpsimd.tensor_copy(out=bias_f32[:], in_=bias_raw[:])

            def w_out_group(b, w_out_raw):
                width = min(WINDOW, D - b * KEEP)
                nc.vector.tensor_copy(
                    out=w_out_grouped[:, b, 0:width, :],
                    in_=w_out_raw[:, :, b * KEEP : b * KEEP + width].rearrange("p j d -> p d j"),
                )

            def w_out_quantise(b):
                nc.vector.quantize_mx(
                    out=w_out_codes[:, b, :].bitcast(FP8X4),
                    scales=w_out_scales[:, b, :],
                    in_=w_out_grouped[:, b].rearrange("p d j -> p (d j)"),
                )

            A, B, C = (0, 1), (2, 3), (4,)
            split_part(0, slice(0, 3))
            split_part(0, slice(3, M2), nc.scalar.copy)
            w_in_group(slice(0, 2), nc.vector.tensor_copy)
            w_in_group(slice(2, PACK), nc.scalar.copy)

            def last_quantise(n):
                if n == 1:
                    quantise_x(TILES - 1, C)
                    for b in range(max(0, TILES - 16), BLOCKS):
                        w_out_group(b, w_out_raw)
                    for b in range(max(0, TILES - 1 - 16), BLOCKS):
                        w_out_quantise(b)

            for h in range(TILES):
                if h + 4 < TILES:
                    load_tile(h + 4)
                if h == 2:
                    w_out_raw = weights.tile([P, PACK, D], BF16)
                    nc.sync.dma_start(
                        out=w_out_raw[:], in_=w_out.rearrange("(p j) d -> p j d", j=PACK)
                    )

                def front(n):
                    if n == 1:
                        transpose_x(h, A)
                        group_x(h, A, nc.vector.tensor_copy)
                        if h > 0:
                            quantise_x(h - 1, C)
                        if h + 1 < TILES:
                            split_part(h + 1, slice(0, 3))
                        quantise_x(h, A)
                        if h == 0:
                            nc.vector.quantize_mx(
                                out=w_in_codes[:].bitcast(FP8X4),
                                scales=w_in_scales[:],
                                in_=w_in_grouped[:].rearrange("p j q i -> p (j q i)"),
                            )
                        if h + 1 < TILES:
                            split_part(h + 1, slice(3, M2))
                        if 16 <= h < 16 + BLOCKS:
                            w_out_group(h - 16, w_out_raw)
                        if 16 + 1 <= h < 16 + 1 + BLOCKS:
                            w_out_quantise(h - 16 - 1)
                    if n == 2:
                        transpose_x(h, B)
                        group_x(h, B, nc.scalar.copy if h < 15 else nc.vector.tensor_copy)
                        transpose_x(h, C)
                        quantise_x(h, B)
                        group_x(h, C, nc.vector.tensor_copy)

                p1_step(h, front)

            p1_step(TILES, last_quantise)
        g_pool = ctx.enter_context(tc.tile_pool(name="g", bufs=2))
        result_pool = ctx.enter_context(tc.tile_pool(name="result", bufs=3))
        pools.extend((g_pool, result_pool))
        take_factor(0)
        sum_squares(14, (0, 1, 2, 3), planes[ADDS(14)])
        take_root(14)

        def last_sum():
            sum_squares(15, (0, 1, 2, 3), planes[ADDS(15)])
            take_root(15)
            take_gelu(2)

        p2_step(0, order=(("h", 0), ("h", 1), ("h", 2), ("h", 3), ("h", 4), ("f", last_sum)), v_extra={4: lambda: take_norm(14)})
        p2_step(1, v_extra={0: lambda: take_norm(15)})
        for i in range(2, TILES + 1):
            p2_step(i)
